import numpy as np
import ml_dtypes


def mxq(x, axis, fmt="e4m3"):
    dtype, down = {"e4m3": (ml_dtypes.float8_e4m3fn, 7), "e5m2": (ml_dtypes.float8_e5m2, 14)}[fmt]
    v = np.moveaxis(np.asarray(x, np.float32).astype(ml_dtypes.bfloat16).astype(np.float64), axis, -1)
    blocks = v.reshape(v.shape[:-1] + (-1, 32))
    amax = np.abs(blocks).max(-1, keepdims=True)
    byte = np.maximum(np.where(amax > 0, np.frexp(amax)[1] - 1 + 127, 0) - down, 1)
    scale = np.exp2(byte - 127.0)
    codes = (blocks / scale).astype(np.float32).astype(dtype).astype(np.float64)
    return np.moveaxis((codes * scale).reshape(v.shape), -1, axis)


WIDE = False


def mx_kscale(k):
    if not WIDE:
        return np.ones(k)
    levels = np.array([20, -20, 10, -10, 0])
    a = np.random.permutation(np.resize(levels, k // 512 * 4)).reshape(k // 512, 4)
    idx = np.arange(k)
    return np.exp2(a[idx // 512, idx % 128 // 32])


BF16 = ml_dtypes.bfloat16


def bf(x):
    return np.asarray(x, np.float32).astype(BF16)


def f64(x):
    return np.asarray(x).astype(np.float64)


B, IN, L = 512, 1536, 1536


def sigmoid(v):
    return 1.0 / (1.0 + np.exp(-v))


def setup_inputs():
    u = mx_kscale(L)
    u3 = np.tile(u, 3)[:, None]
    x = bf(np.random.standard_normal((B, IN)))
    h0 = bf(np.random.standard_normal((B, L)))
    gh0 = bf(np.random.standard_normal((B, 3 * L)) * 0.75)
    w0 = bf(np.random.standard_normal((3 * L, IN)) * 0.7 / np.sqrt(IN))
    b = bf(np.random.standard_normal(3 * L) * 0.3)
    g = bf(np.random.standard_normal((B, L)) * np.exp2(np.random.randint(-12, 1, (B, 1))) * 32.0 * u)
    gi = f64(x) @ f64(w0).T + f64(b)
    gh = f64(gh0)
    r = sigmoid(gi[:, :L] + gh[:, :L])
    z = sigmoid(gi[:, L:2 * L] + gh[:, L:2 * L])
    n = np.tanh(gi[:, 2 * L:] + r * gh[:, 2 * L:])
    return {"input": x, "h0": h0, "gh0": gh0, "W_ih0": bf(f64(w0) / u3), "b_ih0": b,
            "r": np.asarray(r, np.float32), "z": np.asarray(z, np.float32), "n": np.asarray(n, np.float32),
            "grad_out": g}


def reference(input, h0, gh0, W_ih0, b_ih0, r, z, n, grad_out):
    g, h = f64(grad_out), f64(h0)
    h_n = f64(gh0)[:, 2 * L:]
    rf, zf, nf = f64(r), f64(z), f64(n)
    d_n = g * (1.0 - zf) * (1.0 - nf * nf)
    d_z = g * (h - nf) * zf * (1.0 - zf)
    d_r = d_n * h_n * rf * (1.0 - rf)
    dgi = np.concatenate([d_r, d_z, d_n], axis=1)
    return mxq(dgi, 1, "e5m2") @ mxq(f64(W_ih0), 0, "e4m3")

@@ -1,0 +1,253 @@
+from contextlib import ExitStack
+
+import concourse.mybir as mybir
+from concourse.masks import make_identity
+
+F32 = mybir.dt.float32
+BF16 = mybir.dt.bfloat16
+U32 = mybir.dt.uint32
+U8 = mybir.dt.uint8
+E4M3_X4 = mybir.dt.float8_e4m3fn_x4
+E5M2_X4 = mybir.dt.float8_e5m2_x4
+ALU = mybir.AluOpType
+ACT = mybir.ActivationFunctionType
+
+P = 128
+PACK = 4
+K_PASS = P * PACK
+
+BATCH, HIDDEN, N_IN = 512, 1536, 1536
+GATES = 3
+PASSES = GATES * HIDDEN // K_PASS
+BLOCKS = HIDDEN // K_PASS
+ROW_TILES = BATCH // P
+PIECES = ROW_TILES * BLOCKS
+COL_BLOCK = 512
+COL_BLOCKS = N_IN // COL_BLOCK
+
+FIRST_ROW_TILES = 2
+AHEAD = 2
+VECTOR_EVERY = 4
+
+FLOPS = 2 * BATCH * GATES * HIDDEN * N_IN
+BYTES = (
+    2 * GATES * HIDDEN * N_IN
+    + 3 * 4 * BATCH * HIDDEN
+    + 3 * 2 * BATCH * HIDDEN
+    + 4 * BATCH * N_IN
+)
+
+
+def tile_grucellstack_pa_v_kernel(
+    tc, x_in, h0, gh0, w_ih0, b_ih0, r, z, n, grad_out, out
+):
+    nc = tc.nc
+    w_by_pass = w_ih0.rearrange("(c t p) i -> c p t i", t=PACK, p=P)
+
+    with ExitStack() as ctx:
+        keep = ctx.enter_context(tc.tile_pool(name="keep", bufs=1))
+        w_loads = ctx.enter_context(tc.tile_pool(name="w_loads", bufs=AHEAD + 1))
+        w_groups = ctx.enter_context(tc.tile_pool(name="w_groups", bufs=2 * COL_BLOCKS))
+        loads = ctx.enter_context(tc.tile_pool(name="loads", bufs=AHEAD + 1))
+        work = ctx.enter_context(tc.tile_pool(name="work", bufs=2))
+        d_groups = ctx.enter_context(tc.tile_pool(name="d_groups", bufs=2 * GATES))
+        results = ctx.enter_context(tc.tile_pool(name="results", bufs=3))
+        turned = ctx.enter_context(tc.psum_pool(name="turned", bufs=2))
+        banks = ctx.enter_context(tc.psum_pool(name="banks", bufs=FIRST_ROW_TILES * COL_BLOCKS))
+
+        identity = keep.tile([P, P], F32)
+        make_identity(nc, identity[:])
+
+        w_codes = keep.tile([P, PASSES, N_IN], U32, align_bytes=64)
+        w_scales = keep.tile([P, PASSES, N_IN], U8, align_bytes=64)
+        d_codes = keep.tile([P, PASSES, ROW_TILES, P], U32, align_bytes=64)
+        d_scales = keep.tile([P, PASSES, ROW_TILES, P], U8, align_bytes=64)
+
+        w_raw = {}
+        w_grouped = {}
+        piece_in = {}
+        n_squared = {}
+        d_grouped = {}
+        bank_of = {}
+        passes_in = {}
+
+        def load_w(c):
+            raw = w_loads.tile([P, PACK, N_IN], BF16)
+            nc.sync.dma_start(out=raw[:], in_=w_by_pass[c])
+            w_raw[c] = raw
+
+        def load_piece(s):
+            m, q = divmod(s, BLOCKS)
+            rows = slice(m * P, (m + 1) * P)
+            cols = slice(q * K_PASS, (q + 1) * K_PASS)
+            gh_n_cols = slice(2 * HIDDEN + q * K_PASS, 2 * HIDDEN + (q + 1) * K_PASS)
+            z_in = loads.tile([P, K_PASS], F32)
+            nc.sync.dma_start(out=z_in[:], in_=z[rows, cols])
+            g_in = loads.tile([P, K_PASS], BF16)
+            nc.sync.dma_start(out=g_in[:], in_=grad_out[rows, cols])
+            n_in = loads.tile([P, K_PASS], F32)
+            nc.sync.dma_start(out=n_in[:], in_=n[rows, cols])
+            h_in = loads.tile([P, K_PASS], BF16)
+            nc.sync.dma_start(out=h_in[:], in_=h0[rows, cols])
+            r_in = loads.tile([P, K_PASS], F32)
+            nc.sync.dma_start(out=r_in[:], in_=r[rows, cols])
+            gh_n_in = loads.tile([P, K_PASS], BF16)
+            nc.sync.dma_start(out=gh_n_in[:], in_=gh0[rows, gh_n_cols])
+            piece_in[s] = (z_in, g_in, n_in, h_in, r_in, gh_n_in)
+
+        def square_n(s):
+            n_in = piece_in[s][2]
+            n_sq = work.tile([P, K_PASS], F32)
+            nc.scalar.activation(out=n_sq[:], in_=n_in[:], func=ACT.Square)
+            n_squared[s] = n_sq
+
+        def regroup_w(c, j):
+            grouped = w_groups.tile([P, COL_BLOCK, PACK], BF16, align_bytes=64)
+            block = w_raw[c][:, :, j * COL_BLOCK : (j + 1) * COL_BLOCK]
+            src = block.rearrange("p t (a b) -> p a t b", b=4)
+            dst = grouped[:].rearrange("p (a b) t -> p a t b", b=4)
+            if (c * COL_BLOCKS + j) % VECTOR_EVERY == VECTOR_EVERY - 1:
+                nc.vector.tensor_copy(out=dst, in_=src)
+            else:
+                nc.scalar.copy(out=dst, in_=src)
+            w_grouped[(c, j)] = grouped
+
+        def quantise_w(c, j):
+            cols = slice(j * COL_BLOCK, (j + 1) * COL_BLOCK)
+            nc.vector.quantize_mx(
+                out=w_codes[:, c, cols].bitcast(E4M3_X4),
+                scales=w_scales[:, c, cols],
+                in_=w_grouped[(c, j)][:].rearrange("p i t -> p (i t)"),
+            )
+
+        def turn(s, gate, d_gate):
+            bank = turned.tile([P, PACK, P], F32)
+            for t in range(PACK):
+                nc.tensor.transpose(
+                    out=bank[:, t, :], in_=d_gate[:, t * P : (t + 1) * P], identity=identity[:]
+                )
+            grouped = d_groups.tile([P, P, PACK], BF16, align_bytes=64)
+            nc.scalar.copy(out=grouped[:], in_=bank[:].rearrange("p t b -> p b t"))
+            d_grouped[(s, gate)] = grouped
+
+        def quantise_d(s, gate):
+            m, q = divmod(s, BLOCKS)
+            c = gate * BLOCKS + q
+            nc.vector.quantize_mx(
+                out=d_codes[:, c, m, :].bitcast(E5M2_X4),
+                scales=d_scales[:, c, m, :],
+                in_=d_grouped[(s, gate)][:].rearrange("p b t -> p (b t)"),
+            )
+
+        def multiply(c, m, j):
+            if (m, j) not in bank_of:
+                bank = banks.tile([P, COL_BLOCK], F32)
+                bank_of[(m, j)] = bank
+                passes_in[(m, j)] = 0
+            cols = slice(j * COL_BLOCK, (j + 1) * COL_BLOCK)
+            nc.tensor.matmul_mx(
+                out=bank_of[(m, j)][:],
+                lhsT=d_codes[:, c, m, :].bitcast(E5M2_X4),
+                lhsT_scale=d_scales[:, c, m, :],
+                rhs=w_codes[:, c, cols].bitcast(E4M3_X4),
+                rhs_scale=w_scales[:, c, cols],
+                start=(passes_in[(m, j)] == 0),
+                stop=(passes_in[(m, j)] == PASSES - 1),
+            )
+            passes_in[(m, j)] += 1
+
+        def store(m, j):
+            result = results.tile([P, COL_BLOCK], F32)
+            if m == ROW_TILES - 1 and j % 2 == 1:
+                nc.vector.tensor_copy(out=result[:], in_=bank_of[(m, j)][:])
+            else:
+                nc.scalar.copy(out=result[:], in_=bank_of[(m, j)][:])
+            nc.sync.dma_start(
+                out=out[m * P : (m + 1) * P, j * COL_BLOCK : (j + 1) * COL_BLOCK], in_=result[:]
+            )
+
+        def make(s):
+            z_in, g_in, n_in, h_in, r_in, gh_n_in = piece_in[s]
+            if s < PASSES:
+                regroup_w(s, 0)
+            neg_a = work.tile([P, K_PASS], F32)
+            nc.vector.scalar_tensor_tensor(
+                out=neg_a[:], in0=z_in[:], scalar=1.0, in1=g_in[:], op0=ALU.subtract, op1=ALU.mult
+            )
+            n_less_h = work.tile([P, K_PASS], F32)
+            nc.vector.tensor_sub(out=n_less_h[:], in0=n_in[:], in1=h_in[:])
+            neg_rr = work.tile([P, K_PASS], F32)
+            nc.vector.scalar_tensor_tensor(
+                out=neg_rr[:], in0=r_in[:], scalar=1.0, in1=r_in[:], op0=ALU.subtract, op1=ALU.mult
+            )
+            d_n = work.tile([P, K_PASS], F32)
+            nc.vector.scalar_tensor_tensor(
+                out=d_n[:],
+                in0=n_squared[s][:],
+                scalar=1.0,
+                in1=neg_a[:],
+                op0=ALU.subtract,
+                op1=ALU.mult,
+            )
+            turn(s, 2, d_n)
+            if s < PASSES:
+                regroup_w(s, 1)
+            neg_az = work.tile([P, K_PASS], F32)
+            nc.vector.tensor_mul(out=neg_az[:], in0=neg_a[:], in1=z_in[:])
+            d_n_gh = work.tile([P, K_PASS], F32)
+            nc.vector.tensor_mul(out=d_n_gh[:], in0=d_n[:], in1=gh_n_in[:])
+            d_z = work.tile([P, K_PASS], F32)
+            nc.vector.tensor_mul(out=d_z[:], in0=neg_az[:], in1=n_less_h[:])
+            turn(s, 1, d_z)
+            d_r = work.tile([P, K_PASS], F32)
+            nc.vector.scalar_tensor_tensor(
+                out=d_r[:], in0=d_n_gh[:], scalar=-1.0, in1=neg_rr[:], op0=ALU.mult, op1=ALU.mult
+            )
+            turn(s, 0, d_r)
+            if s < PASSES:
+                regroup_w(s, 2)
+
+        def use(s):
+            if s < PASSES:
+                for j in range(COL_BLOCKS):
+                    quantise_w(s, j)
+            for gate in (2, 1, 0):
+                quantise_d(s, gate)
+            for m in range(FIRST_ROW_TILES):
+                for c in range(PASSES):
+                    if max(c, m * BLOCKS + c % BLOCKS) == s:
+                        for j in range(COL_BLOCKS):
+                            multiply(c, m, j)
+            if s == PASSES - 1:
+                for m in range(FIRST_ROW_TILES):
+                    for j in range(COL_BLOCKS):
+                        store(m, j)
+            if PASSES - 1 <= s < PASSES - 1 + COL_BLOCKS:
+                j = s - (PASSES - 1)
+                for c in range(PASSES):
+                    multiply(c, FIRST_ROW_TILES, j)
+                store(FIRST_ROW_TILES, j)
+            if s >= PASSES:
+                m, q = divmod(s, BLOCKS)
+                for gate in (2, 1, 0):
+                    for j in range(COL_BLOCKS):
+                        multiply(gate * BLOCKS + q, m, j)
+            if s == PIECES - 1:
+                for j in range(COL_BLOCKS):
+                    store(ROW_TILES - 1, j)
+
+        for s in range(AHEAD):
+            load_piece(s)
+            load_w(s)
+        square_n(0)
+        for s in range(PIECES + 1):
+            if s + AHEAD < PIECES:
+                load_piece(s + AHEAD)
+            if s + AHEAD < PASSES:
+                load_w(s + AHEAD)
+            if s + 1 < PIECES:
+                square_n(s + 1)
+            if s < PIECES:
+                make(s)
+            if s >= 1:
+                use(s - 1)

@@ -17,6 +17,7 @@ PACK = 4
 K_PASS = P * PACK
 
 BATCH, HIDDEN, N_IN = 512, 1536, 1536
+GATE_R, GATE_Z, GATE_N = 0, 1, 2
 GATES = 3
 PASSES = GATES * HIDDEN // K_PASS
 BLOCKS = HIDDEN // K_PASS
@@ -24,10 +25,13 @@ ROW_TILES = BATCH // P
 PIECES = ROW_TILES * BLOCKS
 COL_BLOCK = 512
 COL_BLOCKS = N_IN // COL_BLOCK
+W_TILES = PASSES * COL_BLOCKS
+LEFT_BLOCKS = 2
+OUT_BANKS = 6
 
-FIRST_ROW_TILES = 2
 AHEAD = 2
-VECTOR_EVERY = 4
+W_TILES_IN_2_STEPS = 5
+VECTOR_EVERY = 5
 
 FLOPS = 2 * BATCH * GATES * HIDDEN * N_IN
 BYTES = (
@@ -38,22 +42,37 @@ BYTES = (
 )
 
 
+def w_tile(i):
+    if i < LEFT_BLOCKS * PASSES:
+        return divmod(i, LEFT_BLOCKS)
+    return i - LEFT_BLOCKS * PASSES, LEFT_BLOCKS
+
+
+def w_tiles_of_step(s):
+    first = W_TILES_IN_2_STEPS * s // 2
+    end = W_TILES_IN_2_STEPS * (s + 1) // 2
+    return [w_tile(i) + (i,) for i in range(first, min(end, W_TILES))]
+
+
 def tile_grucellstack_pa_v_kernel(
     tc, x_in, h0, gh0, w_ih0, b_ih0, r, z, n, grad_out, out
 ):
     nc = tc.nc
     w_by_pass = w_ih0.rearrange("(c t p) i -> c p t i", t=PACK, p=P)
+    left_cols = LEFT_BLOCKS * COL_BLOCK
 
     with ExitStack() as ctx:
         keep = ctx.enter_context(tc.tile_pool(name="keep", bufs=1))
-        w_loads = ctx.enter_context(tc.tile_pool(name="w_loads", bufs=AHEAD + 1))
-        w_groups = ctx.enter_context(tc.tile_pool(name="w_groups", bufs=2 * COL_BLOCKS))
+        w_left = ctx.enter_context(tc.tile_pool(name="w_left", bufs=3))
+        w_right = ctx.enter_context(tc.tile_pool(name="w_right", bufs=5))
+        w_groups = ctx.enter_context(tc.tile_pool(name="w_groups", bufs=6))
         loads = ctx.enter_context(tc.tile_pool(name="loads", bufs=AHEAD + 1))
-        work = ctx.enter_context(tc.tile_pool(name="work", bufs=2))
+        scratch = ctx.enter_context(tc.tile_pool(name="scratch", bufs=1))
+        handed = ctx.enter_context(tc.tile_pool(name="handed", bufs=2))
         d_groups = ctx.enter_context(tc.tile_pool(name="d_groups", bufs=2 * GATES))
-        results = ctx.enter_context(tc.tile_pool(name="results", bufs=3))
+        results = ctx.enter_context(tc.tile_pool(name="results", bufs=4))
         turned = ctx.enter_context(tc.psum_pool(name="turned", bufs=2))
-        banks = ctx.enter_context(tc.psum_pool(name="banks", bufs=FIRST_ROW_TILES * COL_BLOCKS))
+        banks = ctx.enter_context(tc.psum_pool(name="banks", bufs=OUT_BANKS))
 
         identity = keep.tile([P, P], F32)
         make_identity(nc, identity[:])
@@ -65,16 +84,25 @@ def tile_grucellstack_pa_v_kernel(
 
         w_raw = {}
         w_grouped = {}
+        w_made = set()
         piece_in = {}
         n_squared = {}
         d_grouped = {}
+        d_made = set()
         bank_of = {}
         passes_in = {}
+        banks_open = [0]
 
-        def load_w(c):
-            raw = w_loads.tile([P, PACK, N_IN], BF16)
-            nc.sync.dma_start(out=raw[:], in_=w_by_pass[c])
-            w_raw[c] = raw
+        def load_w(c, j):
+            if j == 0:
+                raw = w_left.tile([P, PACK, left_cols], BF16)
+                nc.sync.dma_start(out=raw[:], in_=w_by_pass[c, :, :, 0:left_cols])
+                for b in range(LEFT_BLOCKS):
+                    w_raw[(c, b)] = raw[:, :, b * COL_BLOCK : (b + 1) * COL_BLOCK]
+            if j == LEFT_BLOCKS:
+                raw = w_right.tile([P, PACK, COL_BLOCK], BF16)
+                nc.sync.dma_start(out=raw[:], in_=w_by_pass[c, :, :, left_cols:N_IN])
+                w_raw[(c, j)] = raw[:]
 
         def load_piece(s):
             m, q = divmod(s, BLOCKS)
@@ -97,20 +125,51 @@ def tile_grucellstack_pa_v_kernel(
 
         def square_n(s):
             n_in = piece_in[s][2]
-            n_sq = work.tile([P, K_PASS], F32)
+            n_sq = handed.tile([P, K_PASS], F32)
             nc.scalar.activation(out=n_sq[:], in_=n_in[:], func=ACT.Square)
             n_squared[s] = n_sq
 
-        def regroup_w(c, j):
+        def regroup_w(c, j, i):
             grouped = w_groups.tile([P, COL_BLOCK, PACK], BF16, align_bytes=64)
-            block = w_raw[c][:, :, j * COL_BLOCK : (j + 1) * COL_BLOCK]
-            src = block.rearrange("p t (a b) -> p a t b", b=4)
+            src = w_raw[(c, j)].rearrange("p t (a b) -> p a t b", b=4)
             dst = grouped[:].rearrange("p (a b) t -> p a t b", b=4)
-            if (c * COL_BLOCKS + j) % VECTOR_EVERY == VECTOR_EVERY - 1:
+            if i % VECTOR_EVERY == VECTOR_EVERY - 1:
                 nc.vector.tensor_copy(out=dst, in_=src)
             else:
                 nc.scalar.copy(out=dst, in_=src)
             w_grouped[(c, j)] = grouped
+
+        def store(m, j):
+            result = results.tile([P, COL_BLOCK], F32)
+            if m == ROW_TILES - 1 and j % 2 == 1:
+                nc.vector.tensor_copy(out=result[:], in_=bank_of[(m, j)][:])
+            else:
+                nc.scalar.copy(out=result[:], in_=bank_of[(m, j)][:])
+            nc.sync.dma_start(
+                out=out[m * P : (m + 1) * P, j * COL_BLOCK : (j + 1) * COL_BLOCK], in_=result[:]
+            )
+
+        def multiply(c, m, j):
+            if (m, j) not in bank_of:
+                bank = banks.tile([P, COL_BLOCK], F32)
+                bank_of[(m, j)] = bank
+                passes_in[(m, j)] = 0
+                banks_open[0] += 1
+                assert banks_open[0] <= OUT_BANKS
+            cols = slice(j * COL_BLOCK, (j + 1) * COL_BLOCK)
+            nc.tensor.matmul_mx(
+                out=bank_of[(m, j)][:],
+                lhsT=d_codes[:, c, m, :].bitcast(E5M2_X4),
+                lhsT_scale=d_scales[:, c, m, :],
+                rhs=w_codes[:, c, cols].bitcast(E4M3_X4),
+                rhs_scale=w_scales[:, c, cols],
+                start=(passes_in[(m, j)] == 0),
+                stop=(passes_in[(m, j)] == PASSES - 1),
+            )
+            passes_in[(m, j)] += 1
+            if passes_in[(m, j)] == PASSES:
+                banks_open[0] -= 1
+                store(m, j)
 
         def quantise_w(c, j):
             cols = slice(j * COL_BLOCK, (j + 1) * COL_BLOCK)
@@ -119,6 +178,10 @@ def tile_grucellstack_pa_v_kernel(
                 scales=w_scales[:, c, cols],
                 in_=w_grouped[(c, j)][:].rearrange("p i t -> p (i t)"),
             )
+            w_made.add((c, j))
+            for m in range(ROW_TILES):
+                if (c, m) in d_made:
+                    multiply(c, m, j)
 
         def turn(s, gate, d_gate):
             bank = turned.tile([P, PACK, P], F32)
@@ -138,49 +201,34 @@ def tile_grucellstack_pa_v_kernel(
                 scales=d_scales[:, c, m, :],
                 in_=d_grouped[(s, gate)][:].rearrange("p b t -> p (b t)"),
             )
+            d_made.add((c, m))
+            for j in range(COL_BLOCKS):
+                if (c, j) in w_made:
+                    multiply(c, m, j)
 
-        def multiply(c, m, j):
-            if (m, j) not in bank_of:
-                bank = banks.tile([P, COL_BLOCK], F32)
-                bank_of[(m, j)] = bank
-                passes_in[(m, j)] = 0
-            cols = slice(j * COL_BLOCK, (j + 1) * COL_BLOCK)
-            nc.tensor.matmul_mx(
-                out=bank_of[(m, j)][:],
-                lhsT=d_codes[:, c, m, :].bitcast(E5M2_X4),
-                lhsT_scale=d_scales[:, c, m, :],
-                rhs=w_codes[:, c, cols].bitcast(E4M3_X4),
-                rhs_scale=w_scales[:, c, cols],
-                start=(passes_in[(m, j)] == 0),
-                stop=(passes_in[(m, j)] == PASSES - 1),
-            )
-            passes_in[(m, j)] += 1
+        def make_w(tiles, position):
+            if position < len(tiles):
+                c, j, i = tiles[position]
+                regroup_w(c, j, i)
+                quantise_w(c, j)
 
-        def store(m, j):
-            result = results.tile([P, COL_BLOCK], F32)
-            if m == ROW_TILES - 1 and j % 2 == 1:
-                nc.vector.tensor_copy(out=result[:], in_=bank_of[(m, j)][:])
-            else:
-                nc.scalar.copy(out=result[:], in_=bank_of[(m, j)][:])
-            nc.sync.dma_start(
-                out=out[m * P : (m + 1) * P, j * COL_BLOCK : (j + 1) * COL_BLOCK], in_=result[:]
-            )
-
-        def make(s):
+        def step(s):
+            w_now = w_tiles_of_step(s)
             z_in, g_in, n_in, h_in, r_in, gh_n_in = piece_in[s]
-            if s < PASSES:
-                regroup_w(s, 0)
-            neg_a = work.tile([P, K_PASS], F32)
+            if s + 1 < PIECES:
+                square_n(s + 1)
+            make_w(w_now, 0)
+            neg_a = scratch.tile([P, K_PASS], F32)
             nc.vector.scalar_tensor_tensor(
                 out=neg_a[:], in0=z_in[:], scalar=1.0, in1=g_in[:], op0=ALU.subtract, op1=ALU.mult
             )
-            n_less_h = work.tile([P, K_PASS], F32)
+            n_less_h = scratch.tile([P, K_PASS], F32)
             nc.vector.tensor_sub(out=n_less_h[:], in0=n_in[:], in1=h_in[:])
-            neg_rr = work.tile([P, K_PASS], F32)
+            neg_rr = scratch.tile([P, K_PASS], F32)
             nc.vector.scalar_tensor_tensor(
                 out=neg_rr[:], in0=r_in[:], scalar=1.0, in1=r_in[:], op0=ALU.subtract, op1=ALU.mult
             )
-            d_n = work.tile([P, K_PASS], F32)
+            d_n = handed.tile([P, K_PASS], F32)
             nc.vector.scalar_tensor_tensor(
                 out=d_n[:],
                 in0=n_squared[s][:],
@@ -189,65 +237,35 @@ def tile_grucellstack_pa_v_kernel(
                 op0=ALU.subtract,
                 op1=ALU.mult,
             )
-            turn(s, 2, d_n)
-            if s < PASSES:
-                regroup_w(s, 1)
-            neg_az = work.tile([P, K_PASS], F32)
+            turn(s, GATE_N, d_n)
+            quantise_d(s, GATE_N)
+            make_w(w_now, 1)
+            neg_az = scratch.tile([P, K_PASS], F32)
             nc.vector.tensor_mul(out=neg_az[:], in0=neg_a[:], in1=z_in[:])
-            d_n_gh = work.tile([P, K_PASS], F32)
+            d_n_gh = scratch.tile([P, K_PASS], F32)
             nc.vector.tensor_mul(out=d_n_gh[:], in0=d_n[:], in1=gh_n_in[:])
-            d_z = work.tile([P, K_PASS], F32)
+            d_z = handed.tile([P, K_PASS], F32)
             nc.vector.tensor_mul(out=d_z[:], in0=neg_az[:], in1=n_less_h[:])
-            turn(s, 1, d_z)
-            d_r = work.tile([P, K_PASS], F32)
+            turn(s, GATE_Z, d_z)
+            quantise_d(s, GATE_Z)
+            d_r = handed.tile([P, K_PASS], F32)
             nc.vector.scalar_tensor_tensor(
                 out=d_r[:], in0=d_n_gh[:], scalar=-1.0, in1=neg_rr[:], op0=ALU.mult, op1=ALU.mult
             )
-            turn(s, 0, d_r)
-            if s < PASSES:
-                regroup_w(s, 2)
+            turn(s, GATE_R, d_r)
+            quantise_d(s, GATE_R)
+            make_w(w_now, 2)
 
-        def use(s):
-            if s < PASSES:
-                for j in range(COL_BLOCKS):
-                    quantise_w(s, j)
-            for gate in (2, 1, 0):
-                quantise_d(s, gate)
-            for m in range(FIRST_ROW_TILES):
-                for c in range(PASSES):
-                    if max(c, m * BLOCKS + c % BLOCKS) == s:
-                        for j in range(COL_BLOCKS):
-                            multiply(c, m, j)
-            if s == PASSES - 1:
-                for m in range(FIRST_ROW_TILES):
-                    for j in range(COL_BLOCKS):
-                        store(m, j)
-            if PASSES - 1 <= s < PASSES - 1 + COL_BLOCKS:
-                j = s - (PASSES - 1)
-                for c in range(PASSES):
-                    multiply(c, FIRST_ROW_TILES, j)
-                store(FIRST_ROW_TILES, j)
-            if s >= PASSES:
-                m, q = divmod(s, BLOCKS)
-                for gate in (2, 1, 0):
-                    for j in range(COL_BLOCKS):
-                        multiply(gate * BLOCKS + q, m, j)
-            if s == PIECES - 1:
-                for j in range(COL_BLOCKS):
-                    store(ROW_TILES - 1, j)
-
-        for s in range(AHEAD):
-            load_piece(s)
-            load_w(s)
-        square_n(0)
-        for s in range(PIECES + 1):
-            if s + AHEAD < PIECES:
-                load_piece(s + AHEAD)
-            if s + AHEAD < PASSES:
-                load_w(s + AHEAD)
+        def load_for_step(s):
+            for c, j, i in w_tiles_of_step(s):
+                load_w(c, j)
             if s + 1 < PIECES:
-                square_n(s + 1)
-            if s < PIECES:
-                make(s)
-            if s >= 1:
-                use(s - 1)
+                load_piece(s + 1)
+
+        load_piece(0)
+        for s in range(AHEAD):
+            load_for_step(s)
+        square_n(0)
+        for s in range(PIECES):
+            step(s)
+            load_for_step(s + AHEAD)

@@ -26,12 +26,13 @@ PIECES = ROW_TILES * BLOCKS
 COL_BLOCK = 512
 COL_BLOCKS = N_IN // COL_BLOCK
 W_TILES = PASSES * COL_BLOCKS
-LEFT_BLOCKS = 2
-OUT_BANKS = 6
+FIRST_PART_BLOCKS = 2
+OUT_BANKS = 5
 
-AHEAD = 2
-W_TILES_IN_2_STEPS = 5
-VECTOR_EVERY = 5
+PIECES_AHEAD = 3
+W_LOADS_A_STEP = 2
+W_RAW_TILES = 10
+REGROUP_AHEAD = 2
 
 FLOPS = 2 * BATCH * GATES * HIDDEN * N_IN
 BYTES = (
@@ -43,15 +44,13 @@ BYTES = (
 
 
 def w_tile(i):
-    if i < LEFT_BLOCKS * PASSES:
-        return divmod(i, LEFT_BLOCKS)
-    return i - LEFT_BLOCKS * PASSES, LEFT_BLOCKS
+    j, c = divmod(i, PASSES)
+    return c, j
 
 
 def w_tiles_of_step(s):
-    first = W_TILES_IN_2_STEPS * s // 2
-    end = W_TILES_IN_2_STEPS * (s + 1) // 2
-    return [w_tile(i) + (i,) for i in range(first, min(end, W_TILES))]
+    share = FIRST_PART_BLOCKS * PASSES
+    return [w_tile(i) for i in range(share * s // PIECES, share * (s + 1) // PIECES)]
 
 
 def tile_grucellstack_pa_v_kernel(
@@ -59,19 +58,17 @@ def tile_grucellstack_pa_v_kernel(
 ):
     nc = tc.nc
     w_by_pass = w_ih0.rearrange("(c t p) i -> c p t i", t=PACK, p=P)
-    left_cols = LEFT_BLOCKS * COL_BLOCK
 
     with ExitStack() as ctx:
         keep = ctx.enter_context(tc.tile_pool(name="keep", bufs=1))
-        w_left = ctx.enter_context(tc.tile_pool(name="w_left", bufs=3))
-        w_right = ctx.enter_context(tc.tile_pool(name="w_right", bufs=5))
+        w_loads = ctx.enter_context(tc.tile_pool(name="w_loads", bufs=W_RAW_TILES))
         w_groups = ctx.enter_context(tc.tile_pool(name="w_groups", bufs=6))
-        loads = ctx.enter_context(tc.tile_pool(name="loads", bufs=AHEAD + 1))
+        loads = ctx.enter_context(tc.tile_pool(name="loads", bufs=PIECES_AHEAD))
         scratch = ctx.enter_context(tc.tile_pool(name="scratch", bufs=1))
         handed = ctx.enter_context(tc.tile_pool(name="handed", bufs=2))
         d_groups = ctx.enter_context(tc.tile_pool(name="d_groups", bufs=2 * GATES))
         results = ctx.enter_context(tc.tile_pool(name="results", bufs=4))
-        turned = ctx.enter_context(tc.psum_pool(name="turned", bufs=2))
+        turned = ctx.enter_context(tc.psum_pool(name="turned", bufs=GATES))
         banks = ctx.enter_context(tc.psum_pool(name="banks", bufs=OUT_BANKS))
 
         identity = keep.tile([P, P], F32)
@@ -82,27 +79,29 @@ def tile_grucellstack_pa_v_kernel(
         d_codes = keep.tile([P, PASSES, ROW_TILES, P], U32, align_bytes=64)
         d_scales = keep.tile([P, PASSES, ROW_TILES, P], U8, align_bytes=64)
 
+        w_loaded = [0]
         w_raw = {}
         w_grouped = {}
         w_made = set()
         piece_in = {}
         n_squared = {}
+        turned_bank = {}
         d_grouped = {}
         d_made = set()
+        waiting = [[]]
         bank_of = {}
         passes_in = {}
         banks_open = [0]
 
-        def load_w(c, j):
-            if j == 0:
-                raw = w_left.tile([P, PACK, left_cols], BF16)
-                nc.sync.dma_start(out=raw[:], in_=w_by_pass[c, :, :, 0:left_cols])
-                for b in range(LEFT_BLOCKS):
-                    w_raw[(c, b)] = raw[:, :, b * COL_BLOCK : (b + 1) * COL_BLOCK]
-            if j == LEFT_BLOCKS:
-                raw = w_right.tile([P, PACK, COL_BLOCK], BF16)
-                nc.sync.dma_start(out=raw[:], in_=w_by_pass[c, :, :, left_cols:N_IN])
-                w_raw[(c, j)] = raw[:]
+        def load_next_w():
+            if w_loaded[0] < W_TILES:
+                c, j = w_tile(w_loaded[0])
+                raw = w_loads.tile([P, PACK, COL_BLOCK], BF16)
+                nc.sync.dma_start(
+                    out=raw[:], in_=w_by_pass[c, :, :, j * COL_BLOCK : (j + 1) * COL_BLOCK]
+                )
+                w_raw[(c, j)] = raw
+                w_loaded[0] += 1
 
         def load_piece(s):
             m, q = divmod(s, BLOCKS)
@@ -129,47 +128,15 @@ def tile_grucellstack_pa_v_kernel(
             nc.scalar.activation(out=n_sq[:], in_=n_in[:], func=ACT.Square)
             n_squared[s] = n_sq
 
-        def regroup_w(c, j, i):
+        def regroup_w(c, j, on_vector):
             grouped = w_groups.tile([P, COL_BLOCK, PACK], BF16, align_bytes=64)
-            src = w_raw[(c, j)].rearrange("p t (a b) -> p a t b", b=4)
+            src = w_raw[(c, j)][:].rearrange("p t (a b) -> p a t b", b=4)
             dst = grouped[:].rearrange("p (a b) t -> p a t b", b=4)
-            if i % VECTOR_EVERY == VECTOR_EVERY - 1:
+            if on_vector:
                 nc.vector.tensor_copy(out=dst, in_=src)
             else:
                 nc.scalar.copy(out=dst, in_=src)
             w_grouped[(c, j)] = grouped
-
-        def store(m, j):
-            result = results.tile([P, COL_BLOCK], F32)
-            if m == ROW_TILES - 1 and j % 2 == 1:
-                nc.vector.tensor_copy(out=result[:], in_=bank_of[(m, j)][:])
-            else:
-                nc.scalar.copy(out=result[:], in_=bank_of[(m, j)][:])
-            nc.sync.dma_start(
-                out=out[m * P : (m + 1) * P, j * COL_BLOCK : (j + 1) * COL_BLOCK], in_=result[:]
-            )
-
-        def multiply(c, m, j):
-            if (m, j) not in bank_of:
-                bank = banks.tile([P, COL_BLOCK], F32)
-                bank_of[(m, j)] = bank
-                passes_in[(m, j)] = 0
-                banks_open[0] += 1
-                assert banks_open[0] <= OUT_BANKS
-            cols = slice(j * COL_BLOCK, (j + 1) * COL_BLOCK)
-            nc.tensor.matmul_mx(
-                out=bank_of[(m, j)][:],
-                lhsT=d_codes[:, c, m, :].bitcast(E5M2_X4),
-                lhsT_scale=d_scales[:, c, m, :],
-                rhs=w_codes[:, c, cols].bitcast(E4M3_X4),
-                rhs_scale=w_scales[:, c, cols],
-                start=(passes_in[(m, j)] == 0),
-                stop=(passes_in[(m, j)] == PASSES - 1),
-            )
-            passes_in[(m, j)] += 1
-            if passes_in[(m, j)] == PASSES:
-                banks_open[0] -= 1
-                store(m, j)
 
         def quantise_w(c, j):
             cols = slice(j * COL_BLOCK, (j + 1) * COL_BLOCK)
@@ -181,7 +148,7 @@ def tile_grucellstack_pa_v_kernel(
             w_made.add((c, j))
             for m in range(ROW_TILES):
                 if (c, m) in d_made:
-                    multiply(c, m, j)
+                    waiting[0].append((c, m, j))
 
         def turn(s, gate, d_gate):
             bank = turned.tile([P, PACK, P], F32)
@@ -189,8 +156,11 @@ def tile_grucellstack_pa_v_kernel(
                 nc.tensor.transpose(
                     out=bank[:, t, :], in_=d_gate[:, t * P : (t + 1) * P], identity=identity[:]
                 )
+            turned_bank[(s, gate)] = bank
+
+        def regroup_d(s, gate):
             grouped = d_groups.tile([P, P, PACK], BF16, align_bytes=64)
-            nc.scalar.copy(out=grouped[:], in_=bank[:].rearrange("p t b -> p b t"))
+            nc.scalar.copy(out=grouped[:], in_=turned_bank[(s, gate)][:].rearrange("p t b -> p b t"))
             d_grouped[(s, gate)] = grouped
 
         def quantise_d(s, gate):
@@ -204,20 +174,48 @@ def tile_grucellstack_pa_v_kernel(
             d_made.add((c, m))
             for j in range(COL_BLOCKS):
                 if (c, j) in w_made:
-                    multiply(c, m, j)
+                    waiting[0].append((c, m, j))
 
-        def make_w(tiles, position):
-            if position < len(tiles):
-                c, j, i = tiles[position]
-                regroup_w(c, j, i)
-                quantise_w(c, j)
+        def store(m, j):
+            result = results.tile([P, COL_BLOCK], F32)
+            out_block = out[m * P : (m + 1) * P, j * COL_BLOCK : (j + 1) * COL_BLOCK]
+            if j == COL_BLOCKS - 1 and m % 2 == 1:
+                nc.vector.tensor_copy(out=result[:], in_=bank_of[(m, j)][:])
+                nc.sync.dma_start(out=out_block, in_=result[:])
+            else:
+                nc.scalar.copy(out=result[:], in_=bank_of[(m, j)][:])
+                nc.scalar.dma_start(out=out_block, in_=result[:])
+
+        def multiply_waiting():
+            for c, m, j in waiting[0]:
+                if (m, j) not in bank_of:
+                    bank = banks.tile([P, COL_BLOCK], F32)
+                    bank_of[(m, j)] = bank
+                    passes_in[(m, j)] = 0
+                    banks_open[0] += 1
+                    assert banks_open[0] <= OUT_BANKS
+                cols = slice(j * COL_BLOCK, (j + 1) * COL_BLOCK)
+                nc.tensor.matmul_mx(
+                    out=bank_of[(m, j)][:],
+                    lhsT=d_codes[:, c, m, :].bitcast(E5M2_X4),
+                    lhsT_scale=d_scales[:, c, m, :],
+                    rhs=w_codes[:, c, cols].bitcast(E4M3_X4),
+                    rhs_scale=w_scales[:, c, cols],
+                    start=(passes_in[(m, j)] == 0),
+                    stop=(passes_in[(m, j)] == PASSES - 1),
+                )
+                passes_in[(m, j)] += 1
+                if passes_in[(m, j)] == PASSES:
+                    banks_open[0] -= 1
+                    store(m, j)
+            waiting[0] = []
 
         def step(s):
             w_now = w_tiles_of_step(s)
             z_in, g_in, n_in, h_in, r_in, gh_n_in = piece_in[s]
+            regroup_w(w_now[0][0], w_now[0][1], False)
             if s + 1 < PIECES:
                 square_n(s + 1)
-            make_w(w_now, 0)
             neg_a = scratch.tile([P, K_PASS], F32)
             nc.vector.scalar_tensor_tensor(
                 out=neg_a[:], in0=z_in[:], scalar=1.0, in1=g_in[:], op0=ALU.subtract, op1=ALU.mult
@@ -238,8 +236,9 @@ def tile_grucellstack_pa_v_kernel(
                 op1=ALU.mult,
             )
             turn(s, GATE_N, d_n)
-            quantise_d(s, GATE_N)
-            make_w(w_now, 1)
+            if len(w_now) > 1:
+                regroup_w(w_now[1][0], w_now[1][1], False)
+            regroup_d(s, GATE_N)
             neg_az = scratch.tile([P, K_PASS], F32)
             nc.vector.tensor_mul(out=neg_az[:], in0=neg_a[:], in1=z_in[:])
             d_n_gh = scratch.tile([P, K_PASS], F32)
@@ -247,25 +246,45 @@ def tile_grucellstack_pa_v_kernel(
             d_z = handed.tile([P, K_PASS], F32)
             nc.vector.tensor_mul(out=d_z[:], in0=neg_az[:], in1=n_less_h[:])
             turn(s, GATE_Z, d_z)
-            quantise_d(s, GATE_Z)
             d_r = handed.tile([P, K_PASS], F32)
             nc.vector.scalar_tensor_tensor(
                 out=d_r[:], in0=d_n_gh[:], scalar=-1.0, in1=neg_rr[:], op0=ALU.mult, op1=ALU.mult
             )
             turn(s, GATE_R, d_r)
-            quantise_d(s, GATE_R)
-            make_w(w_now, 2)
+            regroup_d(s, GATE_Z)
+            regroup_d(s, GATE_R)
+            if s > 0:
+                for c, j in w_tiles_of_step(s - 1):
+                    quantise_w(c, j)
+                for gate in (GATE_N, GATE_Z, GATE_R):
+                    quantise_d(s - 1, gate)
+                multiply_waiting()
 
-        def load_for_step(s):
-            for c, j, i in w_tiles_of_step(s):
-                load_w(c, j)
-            if s + 1 < PIECES:
-                load_piece(s + 1)
-
-        load_piece(0)
-        for s in range(AHEAD):
-            load_for_step(s)
+        for s in range(PIECES_AHEAD):
+            load_piece(s)
+            if s + 1 < PIECES_AHEAD:
+                for k in range(W_LOADS_A_STEP):
+                    load_next_w()
         square_n(0)
+
         for s in range(PIECES):
             step(s)
-            load_for_step(s + AHEAD)
+            for k in range(W_LOADS_A_STEP):
+                load_next_w()
+            if s + PIECES_AHEAD < PIECES:
+                load_piece(s + PIECES_AHEAD)
+
+        rest = [w_tile(i) for i in range(FIRST_PART_BLOCKS * PASSES, W_TILES)]
+        for c, j in w_tiles_of_step(PIECES - 1):
+            quantise_w(c, j)
+        for i in range(REGROUP_AHEAD):
+            regroup_w(rest[i][0], rest[i][1], i % 2 == 1)
+        for gate in (GATE_N, GATE_Z, GATE_R):
+            quantise_d(PIECES - 1, gate)
+        multiply_waiting()
+        for i in range(len(rest)):
+            ahead = i + REGROUP_AHEAD
+            if ahead < len(rest):
+                regroup_w(rest[ahead][0], rest[ahead][1], ahead % 2 == 1)
+            quantise_w(rest[i][0], rest[i][1])
+            multiply_waiting()

@@ -57,7 +57,7 @@ def tile_grucellstack_pa_v_kernel(
     tc, x_in, h0, gh0, w_ih0, b_ih0, r, z, n, grad_out, out
 ):
     nc = tc.nc
-    w_by_pass = w_ih0.rearrange("(c t p) i -> c p t i", t=PACK, p=P)
+    w_by_pass = w_ih0.rearrange("(c p t) i -> c p t i", t=PACK, p=P)
 
     with ExitStack() as ctx:
         keep = ctx.enter_context(tc.tile_pool(name="keep", bufs=1))
@@ -66,7 +66,7 @@ def tile_grucellstack_pa_v_kernel(
         loads = ctx.enter_context(tc.tile_pool(name="loads", bufs=PIECES_AHEAD))
         scratch = ctx.enter_context(tc.tile_pool(name="scratch", bufs=1))
         handed = ctx.enter_context(tc.tile_pool(name="handed", bufs=2))
-        d_groups = ctx.enter_context(tc.tile_pool(name="d_groups", bufs=2 * GATES))
+        d_groups = ctx.enter_context(tc.tile_pool(name="d_groups", bufs=3))
         results = ctx.enter_context(tc.tile_pool(name="results", bufs=4))
         turned = ctx.enter_context(tc.psum_pool(name="turned", bufs=GATES))
         banks = ctx.enter_context(tc.psum_pool(name="banks", bufs=OUT_BANKS))
@@ -76,8 +76,8 @@ def tile_grucellstack_pa_v_kernel(
 
         w_codes = keep.tile([P, PASSES, N_IN], U32, align_bytes=64)
         w_scales = keep.tile([P, PASSES, N_IN], U8, align_bytes=64)
-        d_codes = keep.tile([P, PASSES, ROW_TILES, P], U32, align_bytes=64)
-        d_scales = keep.tile([P, PASSES, ROW_TILES, P], U8, align_bytes=64)
+        d_codes = keep.tile([P, PIECES, GATES, P], U32, align_bytes=64)
+        d_scales = keep.tile([P, PIECES, GATES, P], U8, align_bytes=64)
 
         w_loaded = [0]
         w_raw = {}
@@ -85,6 +85,7 @@ def tile_grucellstack_pa_v_kernel(
         w_made = set()
         piece_in = {}
         n_squared = {}
+        r_squared = {}
         turned_bank = {}
         d_grouped = {}
         d_made = set()
@@ -128,6 +129,12 @@ def tile_grucellstack_pa_v_kernel(
             nc.scalar.activation(out=n_sq[:], in_=n_in[:], func=ACT.Square)
             n_squared[s] = n_sq
 
+        def square_r(s):
+            r_in = piece_in[s][4]
+            r_sq = handed.tile([P, K_PASS], F32)
+            nc.scalar.activation(out=r_sq[:], in_=r_in[:], func=ACT.Square, bias=-0.5)
+            r_squared[s] = r_sq
+
         def regroup_w(c, j, on_vector):
             grouped = w_groups.tile([P, COL_BLOCK, PACK], BF16, align_bytes=64)
             src = w_raw[(c, j)][:].rearrange("p t (a b) -> p a t b", b=4)
@@ -150,31 +157,57 @@ def tile_grucellstack_pa_v_kernel(
                 if (c, m) in d_made:
                     waiting[0].append((c, m, j))
 
-        def turn(s, gate, d_gate):
+        def turn_n(s, d_n):
             bank = turned.tile([P, PACK, P], F32)
             for t in range(PACK):
                 nc.tensor.transpose(
-                    out=bank[:, t, :], in_=d_gate[:, t * P : (t + 1) * P], identity=identity[:]
+                    out=bank[:, t, :], in_=d_n[:, t : K_PASS : PACK], identity=identity[:]
                 )
-            turned_bank[(s, gate)] = bank
+            turned_bank[(s, GATE_N)] = bank
 
-        def regroup_d(s, gate):
+        def turn_rz(s, d_rz):
+            bank = turned.tile([P, 2, 2, P], F32)
+            for gate in (GATE_R, GATE_Z):
+                words = d_rz[:, gate, :].bitcast(F32)
+                for u in range(2):
+                    nc.tensor.transpose(
+                        out=bank[:, gate, u, :],
+                        in_=words[:, u : K_PASS // 2 : 2],
+                        identity=identity[:],
+                    )
+            turned_bank[(s, GATE_R)] = bank
+
+        def regroup_n(s):
             grouped = d_groups.tile([P, P, PACK], BF16, align_bytes=64)
-            nc.scalar.copy(out=grouped[:], in_=turned_bank[(s, gate)][:].rearrange("p t b -> p b t"))
-            d_grouped[(s, gate)] = grouped
+            nc.scalar.copy(out=grouped[:], in_=turned_bank[(s, GATE_N)][:].rearrange("p t b -> p b t"))
+            d_grouped[(s, GATE_N)] = grouped
 
-        def quantise_d(s, gate):
-            m, q = divmod(s, BLOCKS)
-            c = gate * BLOCKS + q
-            nc.vector.quantize_mx(
-                out=d_codes[:, c, m, :].bitcast(E5M2_X4),
-                scales=d_scales[:, c, m, :],
-                in_=d_grouped[(s, gate)][:].rearrange("p b t -> p (b t)"),
+        def regroup_rz(s):
+            grouped_rz = d_groups.tile([P, 2, P, PACK], BF16, align_bytes=64)
+            nc.scalar.copy(
+                out=grouped_rz[:].bitcast(F32),
+                in_=turned_bank[(s, GATE_R)][:].rearrange("p g u b -> p g b u"),
             )
-            d_made.add((c, m))
-            for j in range(COL_BLOCKS):
-                if (c, j) in w_made:
-                    waiting[0].append((c, m, j))
+            d_grouped[(s, GATE_R)] = grouped_rz
+
+        def quantise_d(s):
+            m, q = divmod(s, BLOCKS)
+            nc.vector.quantize_mx(
+                out=d_codes[:, s, GATE_N, :].bitcast(E5M2_X4),
+                scales=d_scales[:, s, GATE_N, :],
+                in_=d_grouped[(s, GATE_N)][:].rearrange("p b t -> p (b t)"),
+            )
+            nc.vector.quantize_mx(
+                out=d_codes[:, s, GATE_R : GATE_Z + 1, :].rearrange("p g b -> p (g b)").bitcast(E5M2_X4),
+                scales=d_scales[:, s, GATE_R : GATE_Z + 1, :].rearrange("p g b -> p (g b)"),
+                in_=d_grouped[(s, GATE_R)][:].rearrange("p g b t -> p (g b t)"),
+            )
+            for gate in (GATE_N, GATE_R, GATE_Z):
+                c = gate * BLOCKS + q
+                d_made.add((c, m))
+                for j in range(COL_BLOCKS):
+                    if (c, j) in w_made:
+                        waiting[0].append((c, m, j))
 
         def store(m, j):
             result = results.tile([P, COL_BLOCK], F32)
@@ -197,8 +230,8 @@ def tile_grucellstack_pa_v_kernel(
                 cols = slice(j * COL_BLOCK, (j + 1) * COL_BLOCK)
                 nc.tensor.matmul_mx(
                     out=bank_of[(m, j)][:],
-                    lhsT=d_codes[:, c, m, :].bitcast(E5M2_X4),
-                    lhsT_scale=d_scales[:, c, m, :],
+                    lhsT=d_codes[:, m * BLOCKS + c % BLOCKS, c // BLOCKS, :].bitcast(E5M2_X4),
+                    lhsT_scale=d_scales[:, m * BLOCKS + c % BLOCKS, c // BLOCKS, :],
                     rhs=w_codes[:, c, cols].bitcast(E4M3_X4),
                     rhs_scale=w_scales[:, c, cols],
                     start=(passes_in[(m, j)] == 0),
@@ -216,16 +249,13 @@ def tile_grucellstack_pa_v_kernel(
             regroup_w(w_now[0][0], w_now[0][1], False)
             if s + 1 < PIECES:
                 square_n(s + 1)
+                square_r(s + 1)
             neg_a = scratch.tile([P, K_PASS], F32)
             nc.vector.scalar_tensor_tensor(
                 out=neg_a[:], in0=z_in[:], scalar=1.0, in1=g_in[:], op0=ALU.subtract, op1=ALU.mult
             )
             n_less_h = scratch.tile([P, K_PASS], F32)
             nc.vector.tensor_sub(out=n_less_h[:], in0=n_in[:], in1=h_in[:])
-            neg_rr = scratch.tile([P, K_PASS], F32)
-            nc.vector.scalar_tensor_tensor(
-                out=neg_rr[:], in0=r_in[:], scalar=1.0, in1=r_in[:], op0=ALU.subtract, op1=ALU.mult
-            )
             d_n = handed.tile([P, K_PASS], F32)
             nc.vector.scalar_tensor_tensor(
                 out=d_n[:],
@@ -235,29 +265,32 @@ def tile_grucellstack_pa_v_kernel(
                 op0=ALU.subtract,
                 op1=ALU.mult,
             )
-            turn(s, GATE_N, d_n)
+            turn_n(s, d_n)
             if len(w_now) > 1:
                 regroup_w(w_now[1][0], w_now[1][1], False)
-            regroup_d(s, GATE_N)
+            regroup_n(s)
             neg_az = scratch.tile([P, K_PASS], F32)
             nc.vector.tensor_mul(out=neg_az[:], in0=neg_a[:], in1=z_in[:])
             d_n_gh = scratch.tile([P, K_PASS], F32)
-            nc.vector.tensor_mul(out=d_n_gh[:], in0=d_n[:], in1=gh_n_in[:])
-            d_z = handed.tile([P, K_PASS], F32)
-            nc.vector.tensor_mul(out=d_z[:], in0=neg_az[:], in1=n_less_h[:])
-            turn(s, GATE_Z, d_z)
-            d_r = handed.tile([P, K_PASS], F32)
             nc.vector.scalar_tensor_tensor(
-                out=d_r[:], in0=d_n_gh[:], scalar=-1.0, in1=neg_rr[:], op0=ALU.mult, op1=ALU.mult
+                out=d_n_gh[:], in0=d_n[:], scalar=-1.0, in1=gh_n_in[:], op0=ALU.mult, op1=ALU.mult
             )
-            turn(s, GATE_R, d_r)
-            regroup_d(s, GATE_Z)
-            regroup_d(s, GATE_R)
+            d_rz = handed.tile([P, 2, K_PASS], BF16)
+            nc.vector.tensor_mul(out=d_rz[:, GATE_Z, :], in0=neg_az[:], in1=n_less_h[:])
+            nc.vector.scalar_tensor_tensor(
+                out=d_rz[:, GATE_R, :],
+                in0=r_squared[s][:],
+                scalar=0.25,
+                in1=d_n_gh[:],
+                op0=ALU.subtract,
+                op1=ALU.mult,
+            )
+            turn_rz(s, d_rz)
+            regroup_rz(s)
             if s > 0:
                 for c, j in w_tiles_of_step(s - 1):
                     quantise_w(c, j)
-                for gate in (GATE_N, GATE_Z, GATE_R):
-                    quantise_d(s - 1, gate)
+                quantise_d(s - 1)
                 multiply_waiting()
 
         for s in range(PIECES_AHEAD):
@@ -266,6 +299,7 @@ def tile_grucellstack_pa_v_kernel(
                 for k in range(W_LOADS_A_STEP):
                     load_next_w()
         square_n(0)
+        square_r(0)
 
         for s in range(PIECES):
             step(s)
@@ -279,8 +313,7 @@ def tile_grucellstack_pa_v_kernel(
             quantise_w(c, j)
         for i in range(REGROUP_AHEAD):
             regroup_w(rest[i][0], rest[i][1], i % 2 == 1)
-        for gate in (GATE_N, GATE_Z, GATE_R):
-            quantise_d(PIECES - 1, gate)
+        quantise_d(PIECES - 1)
         multiply_waiting()
         for i in range(len(rest)):
             ahead = i + REGROUP_AHEAD

@@ -33,6 +33,7 @@ PIECES_AHEAD = 3
 W_LOADS_A_STEP = 2
 W_RAW_TILES = 10
 REGROUP_AHEAD = 2
+VECTOR_STEPS = (3, 7, 11)
 
 FLOPS = 2 * BATCH * GATES * HIDDEN * N_IN
 BYTES = (
@@ -267,7 +268,7 @@ def tile_grucellstack_pa_v_kernel(
             )
             turn_n(s, d_n)
             if len(w_now) > 1:
-                regroup_w(w_now[1][0], w_now[1][1], False)
+                regroup_w(w_now[1][0], w_now[1][1], s in VECTOR_STEPS)
             regroup_n(s)
             neg_az = scratch.tile([P, K_PASS], F32)
             nc.vector.tensor_mul(out=neg_az[:], in0=neg_a[:], in1=z_in[:])

@@ -26,14 +26,15 @@ PIECES = ROW_TILES * BLOCKS
 COL_BLOCK = 512
 COL_BLOCKS = N_IN // COL_BLOCK
 W_TILES = PASSES * COL_BLOCKS
-FIRST_PART_BLOCKS = 2
+N_FIRST = 18
+LATE_ON_VECTOR = (0, 1, 3, 5, 7)
 OUT_BANKS = 5
 
 PIECES_AHEAD = 3
 W_LOADS_A_STEP = 2
 W_RAW_TILES = 10
-REGROUP_AHEAD = 2
-VECTOR_STEPS = (3, 7, 11)
+REGROUP_AHEAD = 3
+VECTOR_STEPS = (7,)
 
 FLOPS = 2 * BATCH * GATES * HIDDEN * N_IN
 BYTES = (
@@ -50,8 +51,7 @@ def w_tile(i):
 
 
 def w_tiles_of_step(s):
-    share = FIRST_PART_BLOCKS * PASSES
-    return [w_tile(i) for i in range(share * s // PIECES, share * (s + 1) // PIECES)]
+    return [w_tile(i) for i in range(N_FIRST * s // PIECES, N_FIRST * (s + 1) // PIECES)]
 
 
 def tile_grucellstack_pa_v_kernel(
@@ -71,6 +71,8 @@ def tile_grucellstack_pa_v_kernel(
         results = ctx.enter_context(tc.tile_pool(name="results", bufs=4))
         turned = ctx.enter_context(tc.psum_pool(name="turned", bufs=GATES))
         banks = ctx.enter_context(tc.psum_pool(name="banks", bufs=OUT_BANKS))
+
+        ctx.enter_context(tc.manual_schedule())
 
         identity = keep.tile([P, P], F32)
         make_identity(nc, identity[:])
@@ -221,8 +223,12 @@ def tile_grucellstack_pa_v_kernel(
                 nc.scalar.dma_start(out=out_block, in_=result[:])
 
         def multiply_waiting():
+            later = []
             for c, m, j in waiting[0]:
                 if (m, j) not in bank_of:
+                    if banks_open[0] == OUT_BANKS:
+                        later.append((c, m, j))
+                        continue
                     bank = banks.tile([P, COL_BLOCK], F32)
                     bank_of[(m, j)] = bank
                     passes_in[(m, j)] = 0
@@ -242,7 +248,7 @@ def tile_grucellstack_pa_v_kernel(
                 if passes_in[(m, j)] == PASSES:
                     banks_open[0] -= 1
                     store(m, j)
-            waiting[0] = []
+            waiting[0] = later
 
         def step(s):
             w_now = w_tiles_of_step(s)
@@ -309,16 +315,18 @@ def tile_grucellstack_pa_v_kernel(
             if s + PIECES_AHEAD < PIECES:
                 load_piece(s + PIECES_AHEAD)
 
-        rest = [w_tile(i) for i in range(FIRST_PART_BLOCKS * PASSES, W_TILES)]
+        rest = [w_tile(i) for i in range(N_FIRST, W_TILES)]
         for c, j in w_tiles_of_step(PIECES - 1):
             quantise_w(c, j)
         for i in range(REGROUP_AHEAD):
-            regroup_w(rest[i][0], rest[i][1], i % 2 == 1)
+            regroup_w(rest[i][0], rest[i][1], i in LATE_ON_VECTOR)
         quantise_d(PIECES - 1)
         multiply_waiting()
         for i in range(len(rest)):
             ahead = i + REGROUP_AHEAD
-            if ahead < len(rest):
-                regroup_w(rest[ahead][0], rest[ahead][1], ahead % 2 == 1)
             quantise_w(rest[i][0], rest[i][1])
+            multiply_waiting()
+            if ahead < len(rest):
+                regroup_w(rest[ahead][0], rest[ahead][1], ahead in LATE_ON_VECTOR)
+        for k in range(COL_BLOCKS * ROW_TILES):
             multiply_waiting()

@@ -140,8 +140,8 @@ def tile_grucellstack_pa_v_kernel(
 
         def regroup_w(c, j, on_vector):
             grouped = w_groups.tile([P, COL_BLOCK, PACK], BF16, align_bytes=64)
-            src = w_raw[(c, j)][:].rearrange("p t (a b) -> p a t b", b=4)
-            dst = grouped[:].rearrange("p (a b) t -> p a t b", b=4)
+            src = w_raw[(c, j)][:].rearrange("p t (a b) -> p a t b", b=8)
+            dst = grouped[:].rearrange("p (a b) t -> p a t b", b=8)
             if on_vector:
                 nc.vector.tensor_copy(out=dst, in_=src)
             else:

@@ -68,7 +68,7 @@ def tile_grucellstack_pa_v_kernel(
         scratch = ctx.enter_context(tc.tile_pool(name="scratch", bufs=1))
         handed = ctx.enter_context(tc.tile_pool(name="handed", bufs=2))
         d_groups = ctx.enter_context(tc.tile_pool(name="d_groups", bufs=3))
-        results = ctx.enter_context(tc.tile_pool(name="results", bufs=4))
+        results = ctx.enter_context(tc.tile_pool(name="results", bufs=6))
         turned = ctx.enter_context(tc.psum_pool(name="turned", bufs=GATES))
         banks = ctx.enter_context(tc.psum_pool(name="banks", bufs=OUT_BANKS))
 
@@ -113,17 +113,21 @@ def tile_grucellstack_pa_v_kernel(
             cols = slice(q * K_PASS, (q + 1) * K_PASS)
             gh_n_cols = slice(2 * HIDDEN + q * K_PASS, 2 * HIDDEN + (q + 1) * K_PASS)
             z_in = loads.tile([P, K_PASS], F32)
-            nc.sync.dma_start(out=z_in[:], in_=z[rows, cols])
             g_in = loads.tile([P, K_PASS], BF16)
-            nc.sync.dma_start(out=g_in[:], in_=grad_out[rows, cols])
             n_in = loads.tile([P, K_PASS], F32)
-            nc.sync.dma_start(out=n_in[:], in_=n[rows, cols])
             h_in = loads.tile([P, K_PASS], BF16)
-            nc.sync.dma_start(out=h_in[:], in_=h0[rows, cols])
             r_in = loads.tile([P, K_PASS], F32)
-            nc.sync.dma_start(out=r_in[:], in_=r[rows, cols])
             gh_n_in = loads.tile([P, K_PASS], BF16)
-            nc.sync.dma_start(out=gh_n_in[:], in_=gh0[rows, gh_n_cols])
+            pairs = {
+                "z": (z_in, z[rows, cols]),
+                "g": (g_in, grad_out[rows, cols]),
+                "n": (n_in, n[rows, cols]),
+                "h": (h_in, h0[rows, cols]),
+                "r": (r_in, r[rows, cols]),
+                "gh": (gh_n_in, gh0[rows, gh_n_cols]),
+            }
+            for name in (("z", "g", "n", "h", "r", "gh") if s == 0 else ("n", "r", "z", "g", "h", "gh")):
+                nc.sync.dma_start(out=pairs[name][0][:], in_=pairs[name][1])
             piece_in[s] = (z_in, g_in, n_in, h_in, r_in, gh_n_in)
 
         def square_n(s):
@@ -300,11 +304,13 @@ def tile_grucellstack_pa_v_kernel(
                 quantise_d(s - 1)
                 multiply_waiting()
 
-        for s in range(PIECES_AHEAD):
-            load_piece(s)
-            if s + 1 < PIECES_AHEAD:
-                for k in range(W_LOADS_A_STEP):
-                    load_next_w()
+        load_piece(0)
+        load_next_w()
+        load_piece(1)
+        load_next_w()
+        load_next_w()
+        load_piece(2)
+        load_next_w()
         square_n(0)
         square_r(0)
 

@@ -224,7 +224,7 @@ def tile_grucellstack_pa_v_kernel(
                 nc.sync.dma_start(out=out_block, in_=result[:])
             else:
                 nc.scalar.copy(out=result[:], in_=bank_of[(m, j)][:])
-                nc.scalar.dma_start(out=out_block, in_=result[:])
+                nc.sync.dma_start(out=out_block, in_=result[:])
 
         def multiply_waiting():
             later = []

@@ -26,15 +26,16 @@ PIECES = ROW_TILES * BLOCKS
 COL_BLOCK = 512
 COL_BLOCKS = N_IN // COL_BLOCK
 W_TILES = PASSES * COL_BLOCKS
-N_FIRST = 18
-LATE_ON_VECTOR = (0, 1, 3, 5, 7)
-OUT_BANKS = 5
+OUT_BANKS = 6
+BANKS = 8
 
 PIECES_AHEAD = 3
-W_LOADS_A_STEP = 2
-W_RAW_TILES = 10
-REGROUP_AHEAD = 3
-VECTOR_STEPS = (7,)
+W_LOADS = 14
+W_RAW = 5
+REGROUP_AHEAD = 2
+COUNTS = [2] * 9 + [1, 2, 2]
+ALL_SPLIT = 20
+VECTOR_ROW_TILE = 1
 
 FLOPS = 2 * BATCH * GATES * HIDDEN * N_IN
 BYTES = (
@@ -46,12 +47,14 @@ BYTES = (
 
 
 def w_tile(i):
-    j, c = divmod(i, PASSES)
-    return c, j
+    if i < 2 * PASSES:
+        return i // 2, i % 2
+    return i - 2 * PASSES, 2
 
 
-def w_tiles_of_step(s):
-    return [w_tile(i) for i in range(N_FIRST * s // PIECES, N_FIRST * (s + 1) // PIECES)]
+def tiles_of_step(s):
+    first = sum(COUNTS[:s])
+    return list(range(first, first + COUNTS[s]))
 
 
 def tile_grucellstack_pa_v_kernel(
@@ -62,20 +65,23 @@ def tile_grucellstack_pa_v_kernel(
 
     with ExitStack() as ctx:
         keep = ctx.enter_context(tc.tile_pool(name="keep", bufs=1))
-        w_loads = ctx.enter_context(tc.tile_pool(name="w_loads", bufs=W_RAW_TILES))
+        w_loads = ctx.enter_context(tc.tile_pool(name="w_loads", bufs=W_RAW))
         w_groups = ctx.enter_context(tc.tile_pool(name="w_groups", bufs=6))
         loads = ctx.enter_context(tc.tile_pool(name="loads", bufs=PIECES_AHEAD))
         scratch = ctx.enter_context(tc.tile_pool(name="scratch", bufs=1))
         handed = ctx.enter_context(tc.tile_pool(name="handed", bufs=2))
         d_groups = ctx.enter_context(tc.tile_pool(name="d_groups", bufs=3))
         results = ctx.enter_context(tc.tile_pool(name="results", bufs=6))
-        turned = ctx.enter_context(tc.psum_pool(name="turned", bufs=GATES))
-        banks = ctx.enter_context(tc.psum_pool(name="banks", bufs=OUT_BANKS))
+        psum = ctx.enter_context(tc.psum_pool(name="psum", bufs=1))
 
         ctx.enter_context(tc.manual_schedule())
 
         identity = keep.tile([P, P], F32)
         make_identity(nc, identity[:])
+        neg_identity = keep.tile([P, P], BF16)
+        nc.gpsimd.tensor_scalar(
+            out=neg_identity[:], in0=identity[:], scalar1=-1.0, scalar2=None, op0=ALU.mult
+        )
 
         w_codes = keep.tile([P, PASSES, N_IN], U32, align_bytes=64)
         w_scales = keep.tile([P, PASSES, N_IN], U8, align_bytes=64)
@@ -88,6 +94,8 @@ def tile_grucellstack_pa_v_kernel(
         w_made = set()
         piece_in = {}
         n_squared = {}
+        neg_a_of = {}
+        n_less_h = {}
         r_squared = {}
         turned_bank = {}
         d_grouped = {}
@@ -95,17 +103,32 @@ def tile_grucellstack_pa_v_kernel(
         waiting = [[]]
         bank_of = {}
         passes_in = {}
-        banks_open = [0]
+        full = []
+        to_store = []
+        free_banks = list(range(OUT_BANKS))
+        number_of = {}
 
-        def load_next_w():
-            if w_loaded[0] < W_TILES:
-                c, j = w_tile(w_loaded[0])
-                raw = w_loads.tile([P, PACK, COL_BLOCK], BF16)
-                nc.sync.dma_start(
-                    out=raw[:], in_=w_by_pass[c, :, :, j * COL_BLOCK : (j + 1) * COL_BLOCK]
-                )
-                w_raw[(c, j)] = raw
-                w_loaded[0] += 1
+        def load_w(u):
+            if u < PASSES:
+                raw = w_loads.tile([P, PACK, 2 * COL_BLOCK], BF16)
+                for j in range(2):
+                    w_raw[(u, j)] = raw[:, :, j * COL_BLOCK : (j + 1) * COL_BLOCK]
+                if u == 0:
+                    nc.sync.dma_start(out=w_raw[(u, 0)], in_=w_by_pass[u, :, :, 0:COL_BLOCK])
+                else:
+                    nc.sync.dma_start(out=raw[:], in_=w_by_pass[u, :, :, 0 : 2 * COL_BLOCK])
+            else:
+                raw = w_loads.tile([P, 2, PACK, COL_BLOCK], BF16)
+                first = 2 * (u - PASSES)
+                for c in range(first, min(first + 2, PASSES)):
+                    w_raw[(c, 2)] = raw[:, c - first, :, :]
+                    nc.sync.dma_start(out=w_raw[(c, 2)], in_=w_by_pass[c, :, :, 2 * COL_BLOCK :])
+            w_loaded[0] += 1
+
+        def load_rest_of_first_w():
+            nc.sync.dma_start(
+                out=w_raw[(0, 1)], in_=w_by_pass[0, :, :, COL_BLOCK : 2 * COL_BLOCK]
+            )
 
         def load_piece(s):
             m, q = divmod(s, BLOCKS)
@@ -136,23 +159,35 @@ def tile_grucellstack_pa_v_kernel(
             nc.scalar.activation(out=n_sq[:], in_=n_in[:], func=ACT.Square)
             n_squared[s] = n_sq
 
+        def subtract_h(s):
+            bank = psum.tile([P, K_PASS], F32, name="bank" + str(6 + s % 2))
+            nc.tensor.matmul(
+                out=bank[:], lhsT=identity[:], rhs=piece_in[s][2][:], start=True, stop=False
+            )
+            nc.tensor.matmul(
+                out=bank[:], lhsT=neg_identity[:], rhs=piece_in[s][3][:], start=False, stop=True
+            )
+            n_less_h[s] = bank
+
         def square_r(s):
             r_in = piece_in[s][4]
             r_sq = handed.tile([P, K_PASS], F32)
             nc.scalar.activation(out=r_sq[:], in_=r_in[:], func=ACT.Square, bias=-0.5)
             r_squared[s] = r_sq
 
-        def regroup_w(c, j, on_vector):
-            grouped = w_groups.tile([P, COL_BLOCK, PACK], BF16, align_bytes=64)
-            src = w_raw[(c, j)][:].rearrange("p t (a b) -> p a t b", b=8)
-            dst = grouped[:].rearrange("p (a b) t -> p a t b", b=8)
+        def regroup_w(c, j, lo, hi, on_vector):
+            if (c, j) not in w_grouped:
+                grouped = w_groups.tile([P, COL_BLOCK, PACK], BF16, align_bytes=64)
+                w_grouped[(c, j)] = grouped
+            src = w_raw[(c, j)][:, :, lo:hi].rearrange("p t (a b) -> p a t b", b=8)
+            dst = w_grouped[(c, j)][:, lo:hi, :].rearrange("p (a b) t -> p a t b", b=8)
             if on_vector:
                 nc.vector.tensor_copy(out=dst, in_=src)
             else:
                 nc.scalar.copy(out=dst, in_=src)
-            w_grouped[(c, j)] = grouped
 
-        def quantise_w(c, j):
+        def quantise_w(i):
+            c, j = w_tile(i)
             cols = slice(j * COL_BLOCK, (j + 1) * COL_BLOCK)
             nc.vector.quantize_mx(
                 out=w_codes[:, c, cols].bitcast(E4M3_X4),
@@ -165,7 +200,7 @@ def tile_grucellstack_pa_v_kernel(
                     waiting[0].append((c, m, j))
 
         def turn_n(s, d_n):
-            bank = turned.tile([P, PACK, P], F32)
+            bank = psum.tile([P, PACK, P], F32, name="bank" + str(6 + (s + 1) % 2))
             for t in range(PACK):
                 nc.tensor.transpose(
                     out=bank[:, t, :], in_=d_n[:, t : K_PASS : PACK], identity=identity[:]
@@ -173,7 +208,7 @@ def tile_grucellstack_pa_v_kernel(
             turned_bank[(s, GATE_N)] = bank
 
         def turn_rz(s, d_rz):
-            bank = turned.tile([P, 2, 2, P], F32)
+            bank = psum.tile([P, 2, 2, P], F32, name="bank" + str(6 + s % 2))
             for gate in (GATE_R, GATE_Z):
                 words = d_rz[:, gate, :].bitcast(F32)
                 for u in range(2):
@@ -216,28 +251,37 @@ def tile_grucellstack_pa_v_kernel(
                     if (c, j) in w_made:
                         waiting[0].append((c, m, j))
 
-        def store(m, j):
-            result = results.tile([P, COL_BLOCK], F32)
-            out_block = out[m * P : (m + 1) * P, j * COL_BLOCK : (j + 1) * COL_BLOCK]
-            if j == COL_BLOCKS - 1 and m % 2 == 1:
-                nc.vector.tensor_copy(out=result[:], in_=bank_of[(m, j)][:])
+        def empty_banks(most):
+            for m, j in full[:most]:
+                result = results.tile([P, COL_BLOCK], F32)
+                if m == VECTOR_ROW_TILE:
+                    nc.vector.tensor_copy(out=result[:], in_=bank_of[(m, j)][:])
+                else:
+                    nc.scalar.copy(out=result[:], in_=bank_of[(m, j)][:])
+                free_banks.append(number_of[(m, j)])
+                out_block = out[m * P : (m + 1) * P, j * COL_BLOCK : (j + 1) * COL_BLOCK]
+                to_store.append((out_block, result))
+            for i in range(min(most, len(full))):
+                full.remove(full[0])
+
+        def store_results():
+            for out_block, result in to_store:
                 nc.sync.dma_start(out=out_block, in_=result[:])
-            else:
-                nc.scalar.copy(out=result[:], in_=bank_of[(m, j)][:])
-                nc.sync.dma_start(out=out_block, in_=result[:])
+            to_store.clear()
 
         def multiply_waiting():
             later = []
             for c, m, j in waiting[0]:
                 if (m, j) not in bank_of:
-                    if banks_open[0] == OUT_BANKS:
+                    if not free_banks:
                         later.append((c, m, j))
                         continue
-                    bank = banks.tile([P, COL_BLOCK], F32)
+                    number = free_banks[0]
+                    free_banks.remove(number)
+                    bank = psum.tile([P, COL_BLOCK], F32, name="bank" + str(number))
                     bank_of[(m, j)] = bank
+                    number_of[(m, j)] = number
                     passes_in[(m, j)] = 0
-                    banks_open[0] += 1
-                    assert banks_open[0] <= OUT_BANKS
                 cols = slice(j * COL_BLOCK, (j + 1) * COL_BLOCK)
                 nc.tensor.matmul_mx(
                     out=bank_of[(m, j)][:],
@@ -250,89 +294,112 @@ def tile_grucellstack_pa_v_kernel(
                 )
                 passes_in[(m, j)] += 1
                 if passes_in[(m, j)] == PASSES:
-                    banks_open[0] -= 1
-                    store(m, j)
+                    full.append((m, j))
             waiting[0] = later
 
-        def step(s):
-            w_now = w_tiles_of_step(s)
-            z_in, g_in, n_in, h_in, r_in, gh_n_in = piece_in[s]
-            regroup_w(w_now[0][0], w_now[0][1], False)
-            if s + 1 < PIECES:
-                square_n(s + 1)
-                square_r(s + 1)
+        def start_piece(s):
             neg_a = scratch.tile([P, K_PASS], F32)
             nc.vector.scalar_tensor_tensor(
-                out=neg_a[:], in0=z_in[:], scalar=1.0, in1=g_in[:], op0=ALU.subtract, op1=ALU.mult
-            )
-            n_less_h = scratch.tile([P, K_PASS], F32)
-            nc.vector.tensor_sub(out=n_less_h[:], in0=n_in[:], in1=h_in[:])
-            d_n = handed.tile([P, K_PASS], F32)
-            nc.vector.scalar_tensor_tensor(
-                out=d_n[:],
-                in0=n_squared[s][:],
+                out=neg_a[:],
+                in0=piece_in[s][0][:],
                 scalar=1.0,
-                in1=neg_a[:],
+                in1=piece_in[s][1][:],
                 op0=ALU.subtract,
                 op1=ALU.mult,
             )
+            neg_a_of[s] = neg_a
+
+        def scalar_part(i):
+            return COL_BLOCK // 2 if i >= ALL_SPLIT or i % 2 == 1 else COL_BLOCK
+
+        def regroup_on_scalar(i):
+            c, j = w_tile(i)
+            regroup_w(c, j, 0, scalar_part(i), False)
+
+        def regroup_on_vector(i):
+            c, j = w_tile(i)
+            if scalar_part(i) < COL_BLOCK:
+                regroup_w(c, j, scalar_part(i), COL_BLOCK, True)
+
+        def step(s):
+            z_in, g_in, n_in, h_in, r_in, gh_n_in = piece_in[s]
+            neg_a = neg_a_of[s]
+            empty_banks(4)
+            d_n = handed.tile([P, K_PASS], F32)
+            nc.vector.scalar_tensor_tensor(
+                out=d_n[:], in0=n_squared[s][:], scalar=1.0, in1=neg_a[:], op0=ALU.subtract, op1=ALU.mult
+            )
             turn_n(s, d_n)
-            if len(w_now) > 1:
-                regroup_w(w_now[1][0], w_now[1][1], s in VECTOR_STEPS)
-            regroup_n(s)
+            if s + 1 < PIECES:
+                square_n(s + 1)
+                square_r(s + 1)
             neg_az = scratch.tile([P, K_PASS], F32)
             nc.vector.tensor_mul(out=neg_az[:], in0=neg_a[:], in1=z_in[:])
+            regroup_n(s)
             d_n_gh = scratch.tile([P, K_PASS], F32)
             nc.vector.scalar_tensor_tensor(
                 out=d_n_gh[:], in0=d_n[:], scalar=-1.0, in1=gh_n_in[:], op0=ALU.mult, op1=ALU.mult
             )
+            multiply_waiting()
             d_rz = handed.tile([P, 2, K_PASS], BF16)
-            nc.vector.tensor_mul(out=d_rz[:, GATE_Z, :], in0=neg_az[:], in1=n_less_h[:])
+            nc.vector.tensor_mul(out=d_rz[:, GATE_Z, :], in0=neg_az[:], in1=n_less_h[s][:])
             nc.vector.scalar_tensor_tensor(
-                out=d_rz[:, GATE_R, :],
-                in0=r_squared[s][:],
-                scalar=0.25,
-                in1=d_n_gh[:],
-                op0=ALU.subtract,
-                op1=ALU.mult,
+                out=d_rz[:, GATE_R, :], in0=r_squared[s][:], scalar=0.25, in1=d_n_gh[:], op0=ALU.subtract, op1=ALU.mult
             )
-            turn_rz(s, d_rz)
-            regroup_rz(s)
             if s > 0:
-                for c, j in w_tiles_of_step(s - 1):
-                    quantise_w(c, j)
-                quantise_d(s - 1)
-                multiply_waiting()
+                for i in tiles_of_step(s - 1):
+                    quantise_w(i)
+            turn_rz(s, d_rz)
+            if s + 1 < PIECES:
+                start_piece(s + 1)
+            multiply_waiting()
+            for i in tiles_of_step(s):
+                regroup_on_vector(i)
+            regroup_rz(s)
+            if s + 1 < PIECES:
+                subtract_h(s + 1)
+            quantise_d(s)
+            multiply_waiting()
+            for i in tiles_of_step(s):
+                regroup_on_scalar(i)
 
         load_piece(0)
-        load_next_w()
+        load_w(0)
         load_piece(1)
-        load_next_w()
-        load_next_w()
+        load_rest_of_first_w()
+        load_w(1)
         load_piece(2)
-        load_next_w()
+        start_piece(0)
+        subtract_h(0)
         square_n(0)
         square_r(0)
 
         for s in range(PIECES):
+            store_results()
             step(s)
-            for k in range(W_LOADS_A_STEP):
-                load_next_w()
+            if w_loaded[0] < W_LOADS:
+                load_w(w_loaded[0])
             if s + PIECES_AHEAD < PIECES:
                 load_piece(s + PIECES_AHEAD)
 
-        rest = [w_tile(i) for i in range(N_FIRST, W_TILES)]
-        for c, j in w_tiles_of_step(PIECES - 1):
-            quantise_w(c, j)
-        for i in range(REGROUP_AHEAD):
-            regroup_w(rest[i][0], rest[i][1], i in LATE_ON_VECTOR)
-        quantise_d(PIECES - 1)
+        rest = list(range(sum(COUNTS), W_TILES))
+        for i in rest[:REGROUP_AHEAD]:
+            regroup_on_scalar(i)
+            regroup_on_vector(i)
+        free_banks.extend(range(OUT_BANKS, BANKS))
+        for i in tiles_of_step(PIECES - 1):
+            quantise_w(i)
+        empty_banks(len(full))
         multiply_waiting()
-        for i in range(len(rest)):
-            ahead = i + REGROUP_AHEAD
-            quantise_w(rest[i][0], rest[i][1])
+        for i in rest:
+            quantise_w(i)
+            empty_banks(len(full))
             multiply_waiting()
-            if ahead < len(rest):
-                regroup_w(rest[ahead][0], rest[ahead][1], ahead in LATE_ON_VECTOR)
-        for k in range(COL_BLOCKS * ROW_TILES):
+            store_results()
+            if i + REGROUP_AHEAD < W_TILES:
+                regroup_on_scalar(i + REGROUP_AHEAD)
+                regroup_on_vector(i + REGROUP_AHEAD)
+        while full or waiting[0]:
             multiply_waiting()
+            empty_banks(len(full))
+            store_results()

@@ -329,39 +329,38 @@ def tile_grucellstack_pa_v_kernel(
             nc.vector.scalar_tensor_tensor(
                 out=d_n[:], in0=n_squared[s][:], scalar=1.0, in1=neg_a[:], op0=ALU.subtract, op1=ALU.mult
             )
-            turn_n(s, d_n)
-            if s + 1 < PIECES:
-                square_n(s + 1)
-                square_r(s + 1)
             neg_az = scratch.tile([P, K_PASS], F32)
             nc.vector.tensor_mul(out=neg_az[:], in0=neg_a[:], in1=z_in[:])
+            turn_n(s, d_n)
             regroup_n(s)
+            empty_banks(4)
             d_n_gh = scratch.tile([P, K_PASS], F32)
             nc.vector.scalar_tensor_tensor(
                 out=d_n_gh[:], in0=d_n[:], scalar=-1.0, in1=gh_n_in[:], op0=ALU.mult, op1=ALU.mult
             )
-            multiply_waiting()
             d_rz = handed.tile([P, 2, K_PASS], BF16)
             nc.vector.tensor_mul(out=d_rz[:, GATE_Z, :], in0=neg_az[:], in1=n_less_h[s][:])
             nc.vector.scalar_tensor_tensor(
                 out=d_rz[:, GATE_R, :], in0=r_squared[s][:], scalar=0.25, in1=d_n_gh[:], op0=ALU.subtract, op1=ALU.mult
             )
-            if s > 0:
-                for i in tiles_of_step(s - 1):
-                    quantise_w(i)
-            turn_rz(s, d_rz)
             if s + 1 < PIECES:
-                start_piece(s + 1)
+                square_n(s + 1)
+                square_r(s + 1)
             multiply_waiting()
-            for i in tiles_of_step(s):
-                regroup_on_vector(i)
+            turn_rz(s, d_rz)
             regroup_rz(s)
             if s + 1 < PIECES:
                 subtract_h(s + 1)
-            quantise_d(s)
-            multiply_waiting()
+            if s > 0:
+                for i in tiles_of_step(s - 1):
+                    quantise_w(i)
+            if s + 1 < PIECES:
+                start_piece(s + 1)
             for i in tiles_of_step(s):
                 regroup_on_scalar(i)
+                regroup_on_vector(i)
+            multiply_waiting()
+            quantise_d(s)
 
         load_piece(0)
         load_w(0)
@@ -386,6 +385,7 @@ def tile_grucellstack_pa_v_kernel(
         for i in rest[:REGROUP_AHEAD]:
             regroup_on_scalar(i)
             regroup_on_vector(i)
+        multiply_waiting()
         free_banks.extend(range(OUT_BANKS, BANKS))
         for i in tiles_of_step(PIECES - 1):
             quantise_w(i)

@@ -33,9 +33,11 @@ PIECES_AHEAD = 3
 W_LOADS = 14
 W_RAW = 5
 REGROUP_AHEAD = 2
-COUNTS = [2] * 9 + [1, 2, 2]
-ALL_SPLIT = 20
-VECTOR_ROW_TILE = 1
+TILES_A_STEP = 2
+BUSY_TILE = 18
+LATE_TILES = 22
+LATE_ON_SCALAR = 192
+
 
 FLOPS = 2 * BATCH * GATES * HIDDEN * N_IN
 BYTES = (
@@ -53,15 +55,15 @@ def w_tile(i):
 
 
 def tiles_of_step(s):
-    first = sum(COUNTS[:s])
-    return list(range(first, first + COUNTS[s]))
+    return range(TILES_A_STEP * s, TILES_A_STEP * (s + 1))
 
 
 def tile_grucellstack_pa_v_kernel(
     tc, x_in, h0, gh0, w_ih0, b_ih0, r, z, n, grad_out, out
 ):
     nc = tc.nc
-    w_by_pass = w_ih0.rearrange("(c p t) i -> c p t i", t=PACK, p=P)
+    w_n = w_ih0.rearrange("(c t p) i -> c p t i", t=PACK, p=P)
+    w_rz = w_ih0.rearrange("(c u p e) i -> c u p e i", u=2, e=2, p=P)
 
     with ExitStack() as ctx:
         keep = ctx.enter_context(tc.tile_pool(name="keep", bufs=1))
@@ -108,27 +110,32 @@ def tile_grucellstack_pa_v_kernel(
         free_banks = list(range(OUT_BANKS))
         number_of = {}
 
+        def load_w_cols(c, cols, tile):
+            if c >= GATE_N * BLOCKS:
+                nc.sync.dma_start(out=tile, in_=w_n[c, :, :, cols])
+            else:
+                for u in range(2):
+                    nc.sync.dma_start(out=tile[:, 2 * u : 2 * u + 2, :], in_=w_rz[c, u, :, :, cols])
+
         def load_w(u):
             if u < PASSES:
                 raw = w_loads.tile([P, PACK, 2 * COL_BLOCK], BF16)
                 for j in range(2):
                     w_raw[(u, j)] = raw[:, :, j * COL_BLOCK : (j + 1) * COL_BLOCK]
                 if u == 0:
-                    nc.sync.dma_start(out=w_raw[(u, 0)], in_=w_by_pass[u, :, :, 0:COL_BLOCK])
+                    load_w_cols(0, slice(0, COL_BLOCK), w_raw[(0, 0)])
                 else:
-                    nc.sync.dma_start(out=raw[:], in_=w_by_pass[u, :, :, 0 : 2 * COL_BLOCK])
+                    load_w_cols(u, slice(0, 2 * COL_BLOCK), raw[:])
             else:
                 raw = w_loads.tile([P, 2, PACK, COL_BLOCK], BF16)
                 first = 2 * (u - PASSES)
                 for c in range(first, min(first + 2, PASSES)):
                     w_raw[(c, 2)] = raw[:, c - first, :, :]
-                    nc.sync.dma_start(out=w_raw[(c, 2)], in_=w_by_pass[c, :, :, 2 * COL_BLOCK :])
+                    load_w_cols(c, slice(2 * COL_BLOCK, 3 * COL_BLOCK), w_raw[(c, 2)])
             w_loaded[0] += 1
 
         def load_rest_of_first_w():
-            nc.sync.dma_start(
-                out=w_raw[(0, 1)], in_=w_by_pass[0, :, :, COL_BLOCK : 2 * COL_BLOCK]
-            )
+            load_w_cols(0, slice(COL_BLOCK, 2 * COL_BLOCK), w_raw[(0, 1)])
 
         def load_piece(s):
             m, q = divmod(s, BLOCKS)
@@ -203,7 +210,7 @@ def tile_grucellstack_pa_v_kernel(
             bank = psum.tile([P, PACK, P], F32, name="bank" + str(6 + (s + 1) % 2))
             for t in range(PACK):
                 nc.tensor.transpose(
-                    out=bank[:, t, :], in_=d_n[:, t : K_PASS : PACK], identity=identity[:]
+                    out=bank[:, t, :], in_=d_n[:, t * P : (t + 1) * P], identity=identity[:]
                 )
             turned_bank[(s, GATE_N)] = bank
 
@@ -214,7 +221,7 @@ def tile_grucellstack_pa_v_kernel(
                 for u in range(2):
                     nc.tensor.transpose(
                         out=bank[:, gate, u, :],
-                        in_=words[:, u : K_PASS // 2 : 2],
+                        in_=words[:, u * P : (u + 1) * P],
                         identity=identity[:],
                     )
             turned_bank[(s, GATE_R)] = bank
@@ -254,7 +261,7 @@ def tile_grucellstack_pa_v_kernel(
         def empty_banks(most):
             for m, j in full[:most]:
                 result = results.tile([P, COL_BLOCK], F32)
-                if m == VECTOR_ROW_TILE:
+                if j == COL_BLOCKS - 1 and m % 2 == 1:
                     nc.vector.tensor_copy(out=result[:], in_=bank_of[(m, j)][:])
                 else:
                     nc.scalar.copy(out=result[:], in_=bank_of[(m, j)][:])
@@ -310,11 +317,16 @@ def tile_grucellstack_pa_v_kernel(
             neg_a_of[s] = neg_a
 
         def scalar_part(i):
-            return COL_BLOCK // 2 if i >= ALL_SPLIT or i % 2 == 1 else COL_BLOCK
+            if i == BUSY_TILE:
+                return 0
+            if i >= LATE_TILES:
+                return LATE_ON_SCALAR
+            return COL_BLOCK // 2 if i % 2 == 1 else COL_BLOCK
 
         def regroup_on_scalar(i):
             c, j = w_tile(i)
-            regroup_w(c, j, 0, scalar_part(i), False)
+            if scalar_part(i) > 0:
+                regroup_w(c, j, 0, scalar_part(i), False)
 
         def regroup_on_vector(i):
             c, j = w_tile(i)
@@ -381,7 +393,7 @@ def tile_grucellstack_pa_v_kernel(
             if s + PIECES_AHEAD < PIECES:
                 load_piece(s + PIECES_AHEAD)
 
-        rest = list(range(sum(COUNTS), W_TILES))
+        rest = list(range(TILES_A_STEP * PIECES, W_TILES))
         for i in rest[:REGROUP_AHEAD]:
             regroup_on_scalar(i)
             regroup_on_vector(i)

@@ -34,7 +34,9 @@ W_LOADS = 14
 W_RAW = 5
 REGROUP_AHEAD = 2
 TILES_A_STEP = 2
+HEAD_LOADS = 4
 BUSY_TILE = 18
+AFTER_BUSY = 320
 LATE_TILES = 22
 LATE_ON_SCALAR = 192
 
@@ -137,17 +139,20 @@ def tile_grucellstack_pa_v_kernel(
         def load_rest_of_first_w():
             load_w_cols(0, slice(COL_BLOCK, 2 * COL_BLOCK), w_raw[(0, 1)])
 
-        def load_piece(s):
+        def load_piece(s, first=0, last=6):
             m, q = divmod(s, BLOCKS)
             rows = slice(m * P, (m + 1) * P)
             cols = slice(q * K_PASS, (q + 1) * K_PASS)
             gh_n_cols = slice(2 * HIDDEN + q * K_PASS, 2 * HIDDEN + (q + 1) * K_PASS)
-            z_in = loads.tile([P, K_PASS], F32)
-            g_in = loads.tile([P, K_PASS], BF16)
-            n_in = loads.tile([P, K_PASS], F32)
-            h_in = loads.tile([P, K_PASS], BF16)
-            r_in = loads.tile([P, K_PASS], F32)
-            gh_n_in = loads.tile([P, K_PASS], BF16)
+            if first == 0:
+                z_in = loads.tile([P, K_PASS], F32)
+                g_in = loads.tile([P, K_PASS], BF16)
+                n_in = loads.tile([P, K_PASS], F32)
+                h_in = loads.tile([P, K_PASS], BF16)
+                r_in = loads.tile([P, K_PASS], F32)
+                gh_n_in = loads.tile([P, K_PASS], BF16)
+                piece_in[s] = (z_in, g_in, n_in, h_in, r_in, gh_n_in)
+            z_in, g_in, n_in, h_in, r_in, gh_n_in = piece_in[s]
             pairs = {
                 "z": (z_in, z[rows, cols]),
                 "g": (g_in, grad_out[rows, cols]),
@@ -156,9 +161,8 @@ def tile_grucellstack_pa_v_kernel(
                 "r": (r_in, r[rows, cols]),
                 "gh": (gh_n_in, gh0[rows, gh_n_cols]),
             }
-            for name in (("z", "g", "n", "h", "r", "gh") if s == 0 else ("n", "r", "z", "g", "h", "gh")):
+            for name in (("z", "g", "n", "h", "r", "gh") if s == 0 else ("n", "r", "z", "g", "h", "gh"))[first:last]:
                 nc.sync.dma_start(out=pairs[name][0][:], in_=pairs[name][1])
-            piece_in[s] = (z_in, g_in, n_in, h_in, r_in, gh_n_in)
 
         def square_n(s):
             n_in = piece_in[s][2]
@@ -319,6 +323,8 @@ def tile_grucellstack_pa_v_kernel(
         def scalar_part(i):
             if i == BUSY_TILE:
                 return 0
+            if i == BUSY_TILE + 1:
+                return AFTER_BUSY
             if i >= LATE_TILES:
                 return LATE_ON_SCALAR
             return COL_BLOCK // 2 if i % 2 == 1 else COL_BLOCK
@@ -376,8 +382,9 @@ def tile_grucellstack_pa_v_kernel(
 
         load_piece(0)
         load_w(0)
-        load_piece(1)
+        load_piece(1, 0, HEAD_LOADS)
         load_rest_of_first_w()
+        load_piece(1, HEAD_LOADS, 6)
         load_w(1)
         load_piece(2)
         start_piece(0)

@@ -186,6 +186,10 @@ def tile_grucellstack_pa_v_kernel(
             nc.scalar.activation(out=r_sq[:], in_=r_in[:], func=ACT.Square, bias=-0.5)
             r_squared[s] = r_sq
 
+        def square(s):
+            square_n(s)
+            square_r(s)
+
         def regroup_w(c, j, lo, hi, on_vector):
             if (c, j) not in w_grouped:
                 grouped = w_groups.tile([P, COL_BLOCK, PACK], BF16, align_bytes=64)
@@ -321,13 +325,15 @@ def tile_grucellstack_pa_v_kernel(
             neg_a_of[s] = neg_a
 
         def scalar_part(i):
+            if i == 1:
+                return COL_BLOCK
             if i == BUSY_TILE:
                 return 0
             if i == BUSY_TILE + 1:
                 return AFTER_BUSY
             if i >= LATE_TILES:
                 return LATE_ON_SCALAR
-            return COL_BLOCK // 2 if i % 2 == 1 else COL_BLOCK
+            return COL_BLOCK // 2 if i % 2 == 1 or i == 0 else COL_BLOCK
 
         def regroup_on_scalar(i):
             c, j = w_tile(i)
@@ -350,7 +356,11 @@ def tile_grucellstack_pa_v_kernel(
             neg_az = scratch.tile([P, K_PASS], F32)
             nc.vector.tensor_mul(out=neg_az[:], in0=neg_a[:], in1=z_in[:])
             turn_n(s, d_n)
+            if s == 0:
+                square(1)
             regroup_n(s)
+            if s == 0:
+                regroup_on_scalar(0)
             empty_banks(4)
             d_n_gh = scratch.tile([P, K_PASS], F32)
             nc.vector.scalar_tensor_tensor(
@@ -361,9 +371,8 @@ def tile_grucellstack_pa_v_kernel(
             nc.vector.scalar_tensor_tensor(
                 out=d_rz[:, GATE_R, :], in0=r_squared[s][:], scalar=0.25, in1=d_n_gh[:], op0=ALU.subtract, op1=ALU.mult
             )
-            if s + 1 < PIECES:
-                square_n(s + 1)
-                square_r(s + 1)
+            if 0 < s < PIECES - 1:
+                square(s + 1)
             multiply_waiting()
             turn_rz(s, d_rz)
             regroup_rz(s)
@@ -372,25 +381,29 @@ def tile_grucellstack_pa_v_kernel(
             if s > 0:
                 for i in tiles_of_step(s - 1):
                     quantise_w(i)
+            if s == 1:
+                quantise_d(0)
             if s + 1 < PIECES:
                 start_piece(s + 1)
             for i in tiles_of_step(s):
-                regroup_on_scalar(i)
+                if i > 0:
+                    regroup_on_scalar(i)
                 regroup_on_vector(i)
             multiply_waiting()
-            quantise_d(s)
+            if s > 0:
+                quantise_d(s)
 
         load_piece(0)
-        load_w(0)
         load_piece(1, 0, HEAD_LOADS)
+        load_w(0)
         load_rest_of_first_w()
         load_piece(1, HEAD_LOADS, 6)
+        load_piece(2, 0, HEAD_LOADS)
         load_w(1)
-        load_piece(2)
+        load_piece(2, HEAD_LOADS, 6)
         start_piece(0)
         subtract_h(0)
-        square_n(0)
-        square_r(0)
+        square(0)
 
         for s in range(PIECES):
             store_results()

@@ -35,10 +35,16 @@ W_RAW = 5
 REGROUP_AHEAD = 2
 TILES_A_STEP = 2
 HEAD_LOADS = 4
+WARM_STEPS = 4
+WARM_T = 2
+WARM_B = 0
+TENSOR_SUBTRACTS = 12
+MULT_FROM = 12
+HALF = 256
 BUSY_TILE = 18
 AFTER_BUSY = 320
 LATE_TILES = 22
-LATE_ON_SCALAR = 192
+LATE_ON_SCALAR = 224
 
 
 FLOPS = 2 * BATCH * GATES * HIDDEN * N_IN
@@ -120,14 +126,16 @@ def tile_grucellstack_pa_v_kernel(
                     nc.sync.dma_start(out=tile[:, 2 * u : 2 * u + 2, :], in_=w_rz[c, u, :, :, cols])
 
         def load_w(u):
-            if u < PASSES:
+            if u == 0:
+                raw = w_loads.tile([P, 2, PACK, COL_BLOCK], BF16)
+                for j in range(2):
+                    w_raw[(0, j)] = raw[:, j, :, :]
+                    load_w_cols(0, slice(j * COL_BLOCK, (j + 1) * COL_BLOCK), w_raw[(0, j)])
+            elif u < PASSES:
                 raw = w_loads.tile([P, PACK, 2 * COL_BLOCK], BF16)
                 for j in range(2):
                     w_raw[(u, j)] = raw[:, :, j * COL_BLOCK : (j + 1) * COL_BLOCK]
-                if u == 0:
-                    load_w_cols(0, slice(0, COL_BLOCK), w_raw[(0, 0)])
-                else:
-                    load_w_cols(u, slice(0, 2 * COL_BLOCK), raw[:])
+                load_w_cols(u, slice(0, 2 * COL_BLOCK), raw[:])
             else:
                 raw = w_loads.tile([P, 2, PACK, COL_BLOCK], BF16)
                 first = 2 * (u - PASSES)
@@ -135,9 +143,6 @@ def tile_grucellstack_pa_v_kernel(
                     w_raw[(c, 2)] = raw[:, c - first, :, :]
                     load_w_cols(c, slice(2 * COL_BLOCK, 3 * COL_BLOCK), w_raw[(c, 2)])
             w_loaded[0] += 1
-
-        def load_rest_of_first_w():
-            load_w_cols(0, slice(COL_BLOCK, 2 * COL_BLOCK), w_raw[(0, 1)])
 
         def load_piece(s, first=0, last=6):
             m, q = divmod(s, BLOCKS)
@@ -213,6 +218,14 @@ def tile_grucellstack_pa_v_kernel(
             for m in range(ROW_TILES):
                 if (c, m) in d_made:
                     waiting[0].append((c, m, j))
+
+        def keep_warm(s, count):
+            if s < WARM_STEPS:
+                for i in range(count):
+                    bank = psum.tile([P, COL_BLOCK], F32, name="bank" + str(OUT_BANKS - 1))
+                    nc.tensor.matmul(
+                        out=bank[:], lhsT=neg_identity[:], rhs=piece_in[s][3][:], start=True, stop=True
+                    )
 
         def turn_n(s, d_n):
             bank = psum.tile([P, PACK, P], F32, name="bank" + str(6 + (s + 1) % 2))
@@ -333,7 +346,7 @@ def tile_grucellstack_pa_v_kernel(
                 return AFTER_BUSY
             if i >= LATE_TILES:
                 return LATE_ON_SCALAR
-            return COL_BLOCK // 2 if i % 2 == 1 or i == 0 else COL_BLOCK
+            return HALF if i % 2 == 1 or i == 0 else COL_BLOCK
 
         def regroup_on_scalar(i):
             c, j = w_tile(i)
@@ -356,6 +369,7 @@ def tile_grucellstack_pa_v_kernel(
             neg_az = scratch.tile([P, K_PASS], F32)
             nc.vector.tensor_mul(out=neg_az[:], in0=neg_a[:], in1=z_in[:])
             turn_n(s, d_n)
+            keep_warm(s, WARM_T)
             if s == 0:
                 square(1)
             regroup_n(s)
@@ -376,8 +390,9 @@ def tile_grucellstack_pa_v_kernel(
             multiply_waiting()
             turn_rz(s, d_rz)
             regroup_rz(s)
-            if s + 1 < PIECES:
+            if s + 1 < TENSOR_SUBTRACTS:
                 subtract_h(s + 1)
+            keep_warm(s, WARM_B)
             if s > 0:
                 for i in tiles_of_step(s - 1):
                     quantise_w(i)
@@ -385,6 +400,10 @@ def tile_grucellstack_pa_v_kernel(
                 quantise_d(0)
             if s + 1 < PIECES:
                 start_piece(s + 1)
+            if s + 1 >= TENSOR_SUBTRACTS and s + 1 < PIECES:
+                difference = scratch.tile([P, K_PASS], F32)
+                nc.vector.tensor_sub(out=difference[:], in0=piece_in[s + 1][2][:], in1=piece_in[s + 1][3][:])
+                n_less_h[s + 1] = difference
             for i in tiles_of_step(s):
                 if i > 0:
                     regroup_on_scalar(i)
@@ -392,11 +411,12 @@ def tile_grucellstack_pa_v_kernel(
             multiply_waiting()
             if s > 0:
                 quantise_d(s)
+            if s >= MULT_FROM:
+                multiply_waiting()
 
         load_piece(0)
         load_piece(1, 0, HEAD_LOADS)
         load_w(0)
-        load_rest_of_first_w()
         load_piece(1, HEAD_LOADS, 6)
         load_piece(2, 0, HEAD_LOADS)
         load_w(1)

@@ -39,12 +39,14 @@ WARM_STEPS = 4
 WARM_T = 2
 WARM_B = 0
 TENSOR_SUBTRACTS = 12
-MULT_FROM = 12
+MULT_FROM = 10
 HALF = 256
+LAST_TOGETHER = 2
+EMPTY_FROM = 25
 BUSY_TILE = 18
-AFTER_BUSY = 320
+AFTER_BUSY = 288
 LATE_TILES = 22
-LATE_ON_SCALAR = 224
+LATE_ON_SCALAR = 240
 
 
 FLOPS = 2 * BATCH * GATES * HIDDEN * N_IN
@@ -441,16 +443,20 @@ def tile_grucellstack_pa_v_kernel(
         free_banks.extend(range(OUT_BANKS, BANKS))
         for i in tiles_of_step(PIECES - 1):
             quantise_w(i)
-        empty_banks(len(full))
+        if EMPTY_FROM == 0:
+            empty_banks(len(full))
         multiply_waiting()
         for i in rest:
             quantise_w(i)
-            empty_banks(len(full))
-            multiply_waiting()
+            if i >= EMPTY_FROM:
+                empty_banks(len(full))
+            if i < W_TILES - LAST_TOGETHER:
+                multiply_waiting()
             store_results()
             if i + REGROUP_AHEAD < W_TILES:
                 regroup_on_scalar(i + REGROUP_AHEAD)
                 regroup_on_vector(i + REGROUP_AHEAD)
+        waiting[0] = sorted(waiting[0], key=lambda product: product[1])
         while full or waiting[0]:
             multiply_waiting()
             empty_banks(len(full))

@@ -35,10 +35,6 @@ W_RAW = 5
 REGROUP_AHEAD = 2
 TILES_A_STEP = 2
 HEAD_LOADS = 4
-WARM_STEPS = 4
-WARM_T = 2
-WARM_B = 0
-TENSOR_SUBTRACTS = 12
 MULT_FROM = 10
 HALF = 256
 LAST_TOGETHER = 2
@@ -221,14 +217,6 @@ def tile_grucellstack_pa_v_kernel(
                 if (c, m) in d_made:
                     waiting[0].append((c, m, j))
 
-        def keep_warm(s, count):
-            if s < WARM_STEPS:
-                for i in range(count):
-                    bank = psum.tile([P, COL_BLOCK], F32, name="bank" + str(OUT_BANKS - 1))
-                    nc.tensor.matmul(
-                        out=bank[:], lhsT=neg_identity[:], rhs=piece_in[s][3][:], start=True, stop=True
-                    )
-
         def turn_n(s, d_n):
             bank = psum.tile([P, PACK, P], F32, name="bank" + str(6 + (s + 1) % 2))
             for t in range(PACK):
@@ -371,7 +359,6 @@ def tile_grucellstack_pa_v_kernel(
             neg_az = scratch.tile([P, K_PASS], F32)
             nc.vector.tensor_mul(out=neg_az[:], in0=neg_a[:], in1=z_in[:])
             turn_n(s, d_n)
-            keep_warm(s, WARM_T)
             if s == 0:
                 square(1)
             regroup_n(s)
@@ -392,9 +379,8 @@ def tile_grucellstack_pa_v_kernel(
             multiply_waiting()
             turn_rz(s, d_rz)
             regroup_rz(s)
-            if s + 1 < TENSOR_SUBTRACTS:
+            if s + 1 < PIECES:
                 subtract_h(s + 1)
-            keep_warm(s, WARM_B)
             if s > 0:
                 for i in tiles_of_step(s - 1):
                     quantise_w(i)
@@ -402,10 +388,6 @@ def tile_grucellstack_pa_v_kernel(
                 quantise_d(0)
             if s + 1 < PIECES:
                 start_piece(s + 1)
-            if s + 1 >= TENSOR_SUBTRACTS and s + 1 < PIECES:
-                difference = scratch.tile([P, K_PASS], F32)
-                nc.vector.tensor_sub(out=difference[:], in0=piece_in[s + 1][2][:], in1=piece_in[s + 1][3][:])
-                n_less_h[s + 1] = difference
             for i in tiles_of_step(s):
                 if i > 0:
                     regroup_on_scalar(i)

from contextlib import ExitStack

import concourse.mybir as mybir
from concourse.masks import make_identity

F32 = mybir.dt.float32
BF16 = mybir.dt.bfloat16
U32 = mybir.dt.uint32
U8 = mybir.dt.uint8
E4M3_X4 = mybir.dt.float8_e4m3fn_x4
E5M2_X4 = mybir.dt.float8_e5m2_x4
ALU = mybir.AluOpType
ACT = mybir.ActivationFunctionType

P = 128
PACK = 4
K_PASS = P * PACK

BATCH, HIDDEN, N_IN = 512, 1536, 1536
GATE_R, GATE_Z, GATE_N = 0, 1, 2
GATES = 3
PASSES = GATES * HIDDEN // K_PASS
BLOCKS = HIDDEN // K_PASS
ROW_TILES = BATCH // P
PIECES = ROW_TILES * BLOCKS
COL_BLOCK = 512
COL_BLOCKS = N_IN // COL_BLOCK
W_TILES = PASSES * COL_BLOCKS
OUT_BANKS = 6
BANKS = 8

PIECES_AHEAD = 3
W_LOADS = 14
W_RAW = 5
REGROUP_AHEAD = 2
TILES_A_STEP = 2
HEAD_LOADS = 4
MULT_FROM = 10
HALF = 256
LAST_TOGETHER = 2
EMPTY_FROM = 25
BUSY_TILE = 18
AFTER_BUSY = 288
LATE_TILES = 22
LATE_ON_SCALAR = 240


FLOPS = 2 * BATCH * GATES * HIDDEN * N_IN
BYTES = (
    2 * GATES * HIDDEN * N_IN
    + 3 * 4 * BATCH * HIDDEN
    + 3 * 2 * BATCH * HIDDEN
    + 4 * BATCH * N_IN
)


def w_tile(i):
    if i < 2 * PASSES:
        return i // 2, i % 2
    return i - 2 * PASSES, 2


def tiles_of_step(s):
    return range(TILES_A_STEP * s, TILES_A_STEP * (s + 1))


def tile_grucellstack_pa_v_kernel(
    tc, x_in, h0, gh0, w_ih0, b_ih0, r, z, n, grad_out, out
):
    nc = tc.nc
    w_n = w_ih0.rearrange("(c t p) i -> c p t i", t=PACK, p=P)
    w_rz = w_ih0.rearrange("(c u p e) i -> c u p e i", u=2, e=2, p=P)

    with ExitStack() as ctx:
        keep = ctx.enter_context(tc.tile_pool(name="keep", bufs=1))
        w_loads = ctx.enter_context(tc.tile_pool(name="w_loads", bufs=W_RAW))
        w_groups = ctx.enter_context(tc.tile_pool(name="w_groups", bufs=6))
        loads = ctx.enter_context(tc.tile_pool(name="loads", bufs=PIECES_AHEAD))
        scratch = ctx.enter_context(tc.tile_pool(name="scratch", bufs=1))
        handed = ctx.enter_context(tc.tile_pool(name="handed", bufs=2))
        d_groups = ctx.enter_context(tc.tile_pool(name="d_groups", bufs=3))
        results = ctx.enter_context(tc.tile_pool(name="results", bufs=6))
        psum = ctx.enter_context(tc.psum_pool(name="psum", bufs=1))

        ctx.enter_context(tc.manual_schedule())

        identity = keep.tile([P, P], F32)
        make_identity(nc, identity[:])
        neg_identity = keep.tile([P, P], BF16)
        nc.gpsimd.tensor_scalar(
            out=neg_identity[:], in0=identity[:], scalar1=-1.0, scalar2=None, op0=ALU.mult
        )

        w_codes = keep.tile([P, PASSES, N_IN], U32, align_bytes=64)
        w_scales = keep.tile([P, PASSES, N_IN], U8, align_bytes=64)
        d_codes = keep.tile([P, PIECES, GATES, P], U32, align_bytes=64)
        d_scales = keep.tile([P, PIECES, GATES, P], U8, align_bytes=64)

        w_loaded = [0]
        w_raw = {}
        w_grouped = {}
        w_made = set()
        piece_in = {}
        n_squared = {}
        neg_a_of = {}
        n_less_h = {}
        r_squared = {}
        turned_bank = {}
        d_grouped = {}
        d_made = set()
        waiting = [[]]
        bank_of = {}
        passes_in = {}
        full = []
        to_store = []
        free_banks = list(range(OUT_BANKS))
        number_of = {}

        def load_w_cols(c, cols, tile):
            if c >= GATE_N * BLOCKS:
                nc.sync.dma_start(out=tile, in_=w_n[c, :, :, cols])
            else:
                for u in range(2):
                    nc.sync.dma_start(out=tile[:, 2 * u : 2 * u + 2, :], in_=w_rz[c, u, :, :, cols])

        def load_w(u):
            if u == 0:
                raw = w_loads.tile([P, 2, PACK, COL_BLOCK], BF16)
                for j in range(2):
                    w_raw[(0, j)] = raw[:, j, :, :]
                    load_w_cols(0, slice(j * COL_BLOCK, (j + 1) * COL_BLOCK), w_raw[(0, j)])
            elif u < PASSES:
                raw = w_loads.tile([P, PACK, 2 * COL_BLOCK], BF16)
                for j in range(2):
                    w_raw[(u, j)] = raw[:, :, j * COL_BLOCK : (j + 1) * COL_BLOCK]
                load_w_cols(u, slice(0, 2 * COL_BLOCK), raw[:])
            else:
                raw = w_loads.tile([P, 2, PACK, COL_BLOCK], BF16)
                first = 2 * (u - PASSES)
                for c in range(first, min(first + 2, PASSES)):
                    w_raw[(c, 2)] = raw[:, c - first, :, :]
                    load_w_cols(c, slice(2 * COL_BLOCK, 3 * COL_BLOCK), w_raw[(c, 2)])
            w_loaded[0] += 1

        def load_piece(s, first=0, last=6):
            m, q = divmod(s, BLOCKS)
            rows = slice(m * P, (m + 1) * P)
            cols = slice(q * K_PASS, (q + 1) * K_PASS)
            gh_n_cols = slice(2 * HIDDEN + q * K_PASS, 2 * HIDDEN + (q + 1) * K_PASS)
            if first == 0:
                z_in = loads.tile([P, K_PASS], F32)
                g_in = loads.tile([P, K_PASS], BF16)
                n_in = loads.tile([P, K_PASS], F32)
                h_in = loads.tile([P, K_PASS], BF16)
                r_in = loads.tile([P, K_PASS], F32)
                gh_n_in = loads.tile([P, K_PASS], BF16)
                piece_in[s] = (z_in, g_in, n_in, h_in, r_in, gh_n_in)
            z_in, g_in, n_in, h_in, r_in, gh_n_in = piece_in[s]
            pairs = {
                "z": (z_in, z[rows, cols]),
                "g": (g_in, grad_out[rows, cols]),
                "n": (n_in, n[rows, cols]),
                "h": (h_in, h0[rows, cols]),
                "r": (r_in, r[rows, cols]),
                "gh": (gh_n_in, gh0[rows, gh_n_cols]),
            }
            for name in (("z", "g", "n", "h", "r", "gh") if s == 0 else ("n", "r", "z", "g", "h", "gh"))[first:last]:
                nc.sync.dma_start(out=pairs[name][0][:], in_=pairs[name][1])

        def square_n(s):
            n_in = piece_in[s][2]
            n_sq = handed.tile([P, K_PASS], F32)
            nc.scalar.activation(out=n_sq[:], in_=n_in[:], func=ACT.Square)
            n_squared[s] = n_sq

        def subtract_h(s):
            bank = psum.tile([P, K_PASS], F32, name="bank" + str(6 + s % 2))
            nc.tensor.matmul(
                out=bank[:], lhsT=identity[:], rhs=piece_in[s][2][:], start=True, stop=False
            )
            nc.tensor.matmul(
                out=bank[:], lhsT=neg_identity[:], rhs=piece_in[s][3][:], start=False, stop=True
            )
            n_less_h[s] = bank

        def square_r(s):
            r_in = piece_in[s][4]
            r_sq = handed.tile([P, K_PASS], F32)
            nc.scalar.activation(out=r_sq[:], in_=r_in[:], func=ACT.Square, bias=-0.5)
            r_squared[s] = r_sq

        def square(s):
            square_n(s)
            square_r(s)

        def regroup_w(c, j, lo, hi, on_vector):
            if (c, j) not in w_grouped:
                grouped = w_groups.tile([P, COL_BLOCK, PACK], BF16, align_bytes=64)
                w_grouped[(c, j)] = grouped
            src = w_raw[(c, j)][:, :, lo:hi].rearrange("p t (a b) -> p a t b", b=8)
            dst = w_grouped[(c, j)][:, lo:hi, :].rearrange("p (a b) t -> p a t b", b=8)
            if on_vector:
                nc.vector.tensor_copy(out=dst, in_=src)
            else:
                nc.scalar.copy(out=dst, in_=src)

        def quantise_w(i):
            c, j = w_tile(i)
            cols = slice(j * COL_BLOCK, (j + 1) * COL_BLOCK)
            nc.vector.quantize_mx(
                out=w_codes[:, c, cols].bitcast(E4M3_X4),
                scales=w_scales[:, c, cols],
                in_=w_grouped[(c, j)][:].rearrange("p i t -> p (i t)"),
            )
            w_made.add((c, j))
            for m in range(ROW_TILES):
                if (c, m) in d_made:
                    waiting[0].append((c, m, j))

        def turn_n(s, d_n):
            bank = psum.tile([P, PACK, P], F32, name="bank" + str(6 + (s + 1) % 2))
            for t in range(PACK):
                nc.tensor.transpose(
                    out=bank[:, t, :], in_=d_n[:, t * P : (t + 1) * P], identity=identity[:]
                )
            turned_bank[(s, GATE_N)] = bank

        def turn_rz(s, d_rz):
            bank = psum.tile([P, 2, 2, P], F32, name="bank" + str(6 + s % 2))
            for gate in (GATE_R, GATE_Z):
                words = d_rz[:, gate, :].bitcast(F32)
                for u in range(2):
                    nc.tensor.transpose(
                        out=bank[:, gate, u, :],
                        in_=words[:, u * P : (u + 1) * P],
                        identity=identity[:],
                    )
            turned_bank[(s, GATE_R)] = bank

        def regroup_n(s):
            grouped = d_groups.tile([P, P, PACK], BF16, align_bytes=64)
            nc.scalar.copy(out=grouped[:], in_=turned_bank[(s, GATE_N)][:].rearrange("p t b -> p b t"))
            d_grouped[(s, GATE_N)] = grouped

        def regroup_rz(s):
            grouped_rz = d_groups.tile([P, 2, P, PACK], BF16, align_bytes=64)
            nc.scalar.copy(
                out=grouped_rz[:].bitcast(F32),
                in_=turned_bank[(s, GATE_R)][:].rearrange("p g u b -> p g b u"),
            )
            d_grouped[(s, GATE_R)] = grouped_rz

        def quantise_d(s):
            m, q = divmod(s, BLOCKS)
            nc.vector.quantize_mx(
                out=d_codes[:, s, GATE_N, :].bitcast(E5M2_X4),
                scales=d_scales[:, s, GATE_N, :],
                in_=d_grouped[(s, GATE_N)][:].rearrange("p b t -> p (b t)"),
            )
            nc.vector.quantize_mx(
                out=d_codes[:, s, GATE_R : GATE_Z + 1, :].rearrange("p g b -> p (g b)").bitcast(E5M2_X4),
                scales=d_scales[:, s, GATE_R : GATE_Z + 1, :].rearrange("p g b -> p (g b)"),
                in_=d_grouped[(s, GATE_R)][:].rearrange("p g b t -> p (g b t)"),
            )
            for gate in (GATE_N, GATE_R, GATE_Z):
                c = gate * BLOCKS + q
                d_made.add((c, m))
                for j in range(COL_BLOCKS):
                    if (c, j) in w_made:
                        waiting[0].append((c, m, j))

        def empty_banks(most):
            for m, j in full[:most]:
                result = results.tile([P, COL_BLOCK], F32)
                if j == COL_BLOCKS - 1 and m % 2 == 1:
                    nc.vector.tensor_copy(out=result[:], in_=bank_of[(m, j)][:])
                else:
                    nc.scalar.copy(out=result[:], in_=bank_of[(m, j)][:])
                free_banks.append(number_of[(m, j)])
                out_block = out[m * P : (m + 1) * P, j * COL_BLOCK : (j + 1) * COL_BLOCK]
                to_store.append((out_block, result))
            for i in range(min(most, len(full))):
                full.remove(full[0])

        def store_results():
            for out_block, result in to_store:
                nc.sync.dma_start(out=out_block, in_=result[:])
            to_store.clear()

        def multiply_waiting():
            later = []
            for c, m, j in waiting[0]:
                if (m, j) not in bank_of:
                    if not free_banks:
                        later.append((c, m, j))
                        continue
                    number = free_banks[0]
                    free_banks.remove(number)
                    bank = psum.tile([P, COL_BLOCK], F32, name="bank" + str(number))
                    bank_of[(m, j)] = bank
                    number_of[(m, j)] = number
                    passes_in[(m, j)] = 0
                cols = slice(j * COL_BLOCK, (j + 1) * COL_BLOCK)
                nc.tensor.matmul_mx(
                    out=bank_of[(m, j)][:],
                    lhsT=d_codes[:, m * BLOCKS + c % BLOCKS, c // BLOCKS, :].bitcast(E5M2_X4),
                    lhsT_scale=d_scales[:, m * BLOCKS + c % BLOCKS, c // BLOCKS, :],
                    rhs=w_codes[:, c, cols].bitcast(E4M3_X4),
                    rhs_scale=w_scales[:, c, cols],
                    start=(passes_in[(m, j)] == 0),
                    stop=(passes_in[(m, j)] == PASSES - 1),
                )
                passes_in[(m, j)] += 1
                if passes_in[(m, j)] == PASSES:
                    full.append((m, j))
            waiting[0] = later

        def start_piece(s):
            neg_a = scratch.tile([P, K_PASS], F32)
            nc.vector.scalar_tensor_tensor(
                out=neg_a[:],
                in0=piece_in[s][0][:],
                scalar=1.0,
                in1=piece_in[s][1][:],
                op0=ALU.subtract,
                op1=ALU.mult,
            )
            neg_a_of[s] = neg_a

        def scalar_part(i):
            if i == 1:
                return COL_BLOCK
            if i == BUSY_TILE:
                return 0
            if i == BUSY_TILE + 1:
                return AFTER_BUSY
            if i >= LATE_TILES:
                return LATE_ON_SCALAR
            return HALF if i % 2 == 1 or i == 0 else COL_BLOCK

        def regroup_on_scalar(i):
            c, j = w_tile(i)
            if scalar_part(i) > 0:
                regroup_w(c, j, 0, scalar_part(i), False)

        def regroup_on_vector(i):
            c, j = w_tile(i)
            if scalar_part(i) < COL_BLOCK:
                regroup_w(c, j, scalar_part(i), COL_BLOCK, True)

        def step(s):
            z_in, g_in, n_in, h_in, r_in, gh_n_in = piece_in[s]
            neg_a = neg_a_of[s]
            empty_banks(4)
            d_n = handed.tile([P, K_PASS], F32)
            nc.vector.scalar_tensor_tensor(
                out=d_n[:], in0=n_squared[s][:], scalar=1.0, in1=neg_a[:], op0=ALU.subtract, op1=ALU.mult
            )
            neg_az = scratch.tile([P, K_PASS], F32)
            nc.vector.tensor_mul(out=neg_az[:], in0=neg_a[:], in1=z_in[:])
            turn_n(s, d_n)
            if s == 0:
                square(1)
            regroup_n(s)
            if s == 0:
                regroup_on_scalar(0)
            empty_banks(4)
            d_n_gh = scratch.tile([P, K_PASS], F32)
            nc.vector.scalar_tensor_tensor(
                out=d_n_gh[:], in0=d_n[:], scalar=-1.0, in1=gh_n_in[:], op0=ALU.mult, op1=ALU.mult
            )
            d_rz = handed.tile([P, 2, K_PASS], BF16)
            nc.vector.tensor_mul(out=d_rz[:, GATE_Z, :], in0=neg_az[:], in1=n_less_h[s][:])
            nc.vector.scalar_tensor_tensor(
                out=d_rz[:, GATE_R, :], in0=r_squared[s][:], scalar=0.25, in1=d_n_gh[:], op0=ALU.subtract, op1=ALU.mult
            )
            if 0 < s < PIECES - 1:
                square(s + 1)
            multiply_waiting()
            turn_rz(s, d_rz)
            regroup_rz(s)
            if s + 1 < PIECES:
                subtract_h(s + 1)
            if s > 0:
                for i in tiles_of_step(s - 1):
                    quantise_w(i)
            if s == 1:
                quantise_d(0)
            if s + 1 < PIECES:
                start_piece(s + 1)
            for i in tiles_of_step(s):
                if i > 0:
                    regroup_on_scalar(i)
                regroup_on_vector(i)
            multiply_waiting()
            if s > 0:
                quantise_d(s)
            if s >= MULT_FROM:
                multiply_waiting()

        load_piece(0)
        load_piece(1, 0, HEAD_LOADS)
        load_w(0)
        load_piece(1, HEAD_LOADS, 6)
        load_piece(2, 0, HEAD_LOADS)
        load_w(1)
        load_piece(2, HEAD_LOADS, 6)
        start_piece(0)
        subtract_h(0)
        square(0)

        for s in range(PIECES):
            store_results()
            step(s)
            if w_loaded[0] < W_LOADS:
                load_w(w_loaded[0])
            if s + PIECES_AHEAD < PIECES:
                load_piece(s + PIECES_AHEAD)

        rest = list(range(TILES_A_STEP * PIECES, W_TILES))
        for i in rest[:REGROUP_AHEAD]:
            regroup_on_scalar(i)
            regroup_on_vector(i)
        multiply_waiting()
        free_banks.extend(range(OUT_BANKS, BANKS))
        for i in tiles_of_step(PIECES - 1):
            quantise_w(i)
        if EMPTY_FROM == 0:
            empty_banks(len(full))
        multiply_waiting()
        for i in rest:
            quantise_w(i)
            if i >= EMPTY_FROM:
                empty_banks(len(full))
            if i < W_TILES - LAST_TOGETHER:
                multiply_waiting()
            store_results()
            if i + REGROUP_AHEAD < W_TILES:
                regroup_on_scalar(i + REGROUP_AHEAD)
                regroup_on_vector(i + REGROUP_AHEAD)
        waiting[0] = sorted(waiting[0], key=lambda product: product[1])
        while full or waiting[0]:
            multiply_waiting()
            empty_banks(len(full))
            store_results()
